import numpy as np
import ml_dtypes


def mxq(x, axis, fmt="e4m3"):
    dtype, down = {"e4m3": (ml_dtypes.float8_e4m3fn, 7), "e5m2": (ml_dtypes.float8_e5m2, 14)}[fmt]
    v = np.moveaxis(np.asarray(x, np.float32).astype(ml_dtypes.bfloat16).astype(np.float64), axis, -1)
    blocks = v.reshape(v.shape[:-1] + (-1, 32))
    amax = np.abs(blocks).max(-1, keepdims=True)
    byte = np.maximum(np.where(amax > 0, np.frexp(amax)[1] - 1 + 127, 0) - down, 1)
    scale = np.exp2(byte - 127.0)
    codes = (blocks / scale).astype(np.float32).astype(dtype).astype(np.float64)
    return np.moveaxis((codes * scale).reshape(v.shape), -1, axis)


WIDE = False


def mx_kscale(k):
    if not WIDE:
        return np.ones(k)
    levels = np.array([10, -10, 5, -5, 0])
    if k % 512:
        return np.exp2(np.random.permutation(np.resize(levels, k // 32))).repeat(32)
    a = np.empty((k // 512, 16))
    for p in range(k // 512):
        a[p, :8] = np.random.permutation(np.resize(levels, 8))
        for g in range(8):
            far = levels[np.abs(levels - a[p, g]) >= 10]
            a[p, g + 8] = far[np.random.randint(len(far))]
    return np.exp2(a.ravel()).repeat(32)


BF16 = ml_dtypes.bfloat16


def bf(x):
    return np.asarray(x, np.float32).astype(BF16)


def f64(x):
    return np.asarray(x).astype(np.float64)


B, H, S, D, W = 1, 2, 2048, 128, 512
NEG = -1e9


def setup_inputs():
    t = mx_kscale(W)
    t = np.roll(t, -np.argmax(t))
    s = np.tile(t, S // W)
    q = np.random.standard_normal((B, H, S, D)) * 2.0
    k = np.random.standard_normal((B, H, S, D))
    v = np.random.standard_normal((B, H, S, D))
    q[..., 0] = 8.0
    k[..., 0] += np.log(s) * np.sqrt(D) / 8.0
    v = v * (s.max() / s)[:, None]
    return {"q": bf(q), "k": bf(k), "v": bf(v), "layer_idx": 1}


def reference(q, k, v, layer_idx):
    q, k = f64(q), f64(k)
    vq = mxq(f64(v), 2, "e4m3")
    out = np.zeros((B, H, S, D))
    for i0 in range(0, S, W):
        i1 = i0 + W
        j0 = 0 if layer_idx % 2 == 0 else max(i0 - W, 0)
        s = q[:, :, i0:i1] @ k[:, :, j0:i1].transpose(0, 1, 3, 2) / np.sqrt(D)
        i = np.arange(i0, i1)[:, None]
        j = np.arange(j0, i1)[None, :]
        mask = j <= i
        if layer_idx % 2 != 0:
            mask = mask & (j > i - W)
        s = np.where(mask, s, NEG)
        e = np.exp(s - s.max(-1, keepdims=True))
        out[:, :, i0:i1] = (mxq(e, 3, "e4m3") @ vq[:, :, j0:i1]) / e.sum(-1, keepdims=True)
    return out

@@ -1,0 +1,310 @@
+from contextlib import ExitStack
+import math
+
+import concourse.mybir as mybir
+from concourse.masks import make_identity
+
+F32 = mybir.dt.float32
+BF16 = mybir.dt.bfloat16
+U32 = mybir.dt.uint32
+U8 = mybir.dt.uint8
+FP8X4 = mybir.dt.float8_e4m3fn_x4
+ALU = mybir.AluOpType
+ACT = mybir.ActivationFunctionType
+AX = mybir.AxisListType
+
+H, S, D, W = 2, 2048, 128, 512
+P = 128
+HT = P // 2
+NT = S // P
+TPC = W // P
+NCH = S // W
+NQ = H * NT
+SCALE = 1.0 / math.sqrt(D)
+MASKED = -17179869184.0
+FLOPS = 2 * 2 * H * D * (W * W + (NCH - 1) * W * 2 * W)
+
+
+def tile_multiheadattn_kernel(tc, q, k, v, layer_idx, out):
+    assert layer_idx % 2 == 1, "only the local mask of the odd layers is built"
+    nc = tc.nc
+    qv = q.rearrange("b h (n p) d -> (b h) p n d", p=P)
+    kv = k.rearrange("b h (n p) d -> (b h) p n d", p=P)
+    vv = v.rearrange("b h (g p t) d -> (b h) p g t d", p=P, t=TPC)
+    ov = out.rearrange("b h (n p) d -> (b h) p n d", p=P)
+
+    tiles = [(0, n) for n in range(NT)] + [(1, n) for n in range(NT - 1, -1, -1)]
+    chunks = [(0, c) for c in range(NCH)] + [(1, c) for c in range(NCH - 1, -1, -1)]
+
+    with ExitStack() as ctx:
+        keep = ctx.enter_context(tc.tile_pool(name="keep", bufs=1))
+        small = ctx.enter_context(tc.tile_pool(name="small", bufs=10))
+        gpool = ctx.enter_context(tc.tile_pool(name="gpool", bufs=3))
+        cpool = ctx.enter_context(tc.tile_pool(name="cpool", bufs=3))
+        opool = ctx.enter_context(tc.tile_pool(name="opool", bufs=4))
+        ps_a = ctx.enter_context(tc.psum_pool(name="ps_a", bufs=3))
+        ps_d = ctx.enter_context(tc.psum_pool(name="ps_d", bufs=2))
+        ps_t = ctx.enter_context(tc.psum_pool(name="ps_t", bufs=2))
+        ps_o = ctx.enter_context(tc.psum_pool(name="ps_o", bufs=1))
+        ctx.enter_context(tc.manual_schedule())
+
+        q_raw = keep.tile([P, H, NT, D], BF16)
+        k_raw = keep.tile([P, H, NT, D], BF16)
+        v_raw = keep.tile([P, H, NCH, TPC, D], BF16)
+        qT = keep.tile([P, H, S], BF16)
+        kT = keep.tile([P, H, 2, S // 2], BF16)
+        v_grp = keep.tile([P, H, NCH, D, TPC], BF16, align_bytes=64)
+        v_cod = keep.tile([P, H, NCH * D], U32, align_bytes=64)
+        v_scl = keep.tile([P, H, NCH * D], U8, align_bytes=64)
+        ident = keep.tile([P, P], BF16)
+        ident_w = keep.tile([P, P], F32)
+        mask_f = keep.tile([P, 2, P], F32)
+        mask_b = keep.tile([P, 2, P], BF16)
+        warm = keep.tile([P, 2], F32)
+        rs = keep.tile([P, NQ, 2], F32)
+        e_fix = []
+        for h in range(H):
+            for r in range(TPC):
+                e_hr = keep.tile([P, 2, W], BF16, name="e%d%d" % (h, r))
+                e_fix.append(e_hr)
+
+        def load(queue, raw, view, h, c):
+            queue.dma_start(out=raw[:, h, c * TPC:(c + 1) * TPC, :], in_=view[h][:, c * TPC:(c + 1) * TPC, :])
+
+        load(nc.sync, k_raw, kv, 0, 0)
+        load(nc.scalar, q_raw, qv, 0, 0)
+        for g in range(NCH):
+            nc.sync.dma_start(out=v_raw[:, 0, g], in_=vv[0][:, g])
+        for x, (h, c) in enumerate(chunks):
+            if x > 0:
+                load(nc.sync, k_raw, kv, h, c)
+                load(nc.sync, q_raw, qv, h, c)
+            if x == NCH:
+                nc.sync.dma_start(out=v_raw[:, 1], in_=vv[1])
+
+        make_identity(nc, ident[:])
+        make_identity(nc, ident_w[:])
+        nc.vector.memset(warm[:, 0:1], 0.0)
+        nc.scalar.activation(out=warm[:, 1:2], in_=warm[:, 0:1], func=ACT.Exp)
+        nc.gpsimd.memset(mask_f[:], 0.0)
+        nc.gpsimd.affine_select(out=mask_f[:, 0, :], in_=mask_f[:, 0, :], compare_op=ALU.is_ge, fill=MASKED,
+                                base=0, pattern=[[-1, P]], channel_multiplier=1)
+        nc.gpsimd.affine_select(out=mask_f[:, 1, :], in_=mask_f[:, 1, :], compare_op=ALU.is_ge, fill=MASKED,
+                                base=-1, pattern=[[1, P]], channel_multiplier=-1)
+        for h in range(H):
+            for r in range(TPC):
+                e_hr = e_fix[h * TPC + r]
+                if r > 0:
+                    nc.gpsimd.memset(e_hr[:, :, 0:HT * r], 0.0)
+                if r < TPC - 1:
+                    nc.gpsimd.memset(e_hr[:, :, HT * (r + TPC + 1):W], 0.0)
+        nc.vector.memset(rs[:], 0.0)
+        for y in range(2):
+            nc.vector.tensor_copy(out=mask_b[:, y, :].rearrange("p (u w i) -> p u w i", u=2, i=2),
+                                  in_=mask_f[:, y, :].rearrange("p (w u i) -> p u w i", u=2, i=2))
+
+        live = {}
+
+        def transpose_qk(h, c):
+            tp = ps_t.tile([P, 2 * TPC, P], BF16, tag="tp")
+            live["tp", h, c] = tp
+            for j in range(TPC):
+                nc.tensor.transpose(tp[:, j, :], q_raw[:, h, c * TPC + j, :], ident[:])
+            for j in range(TPC):
+                nc.tensor.transpose(tp[:, TPC + j, :], k_raw[:, h, c * TPC + j, :], ident[:])
+
+        def copy_qk(h, c):
+            tp = live["tp", h, c]
+            nc.vector.tensor_copy(out=qT[:, h, c * W:(c + 1) * W], in_=tp[:, 0:TPC, :].rearrange("p j s -> p (j s)"))
+            keys = tp[:, TPC:2 * TPC, :].rearrange("p j s -> p (j s)")
+            nc.vector.tensor_copy(
+                out=kT[:, h, :, c * TPC * HT:(c + 1) * TPC * HT].rearrange("p u (w i) -> p u w i", i=2),
+                in_=keys.rearrange("p (w u i) -> p u w i", u=2, i=2))
+
+        def regroup_v(h, g):
+            dst = v_grp[:, h, g].rearrange("p (c i) t -> p c t i", i=4)
+            src = v_raw[:, h, g].rearrange("p t (c i) -> p c t i", i=4)
+            if h == 0:
+                nc.scalar.copy(out=dst, in_=src)
+            else:
+                nc.vector.tensor_copy(out=dst, in_=src)
+
+        def quantise_v(h, g):
+            nc.vector.quantize_mx(out=v_cod[:, h, g * D:(g + 1) * D].bitcast(FP8X4),
+                                  scales=v_scl[:, h, g * D:(g + 1) * D],
+                                  in_=v_grp[:, h, g].rearrange("p d t -> p (d t)"))
+
+        def diagonal_scores(h, c):
+            dg = ps_d.tile([P, TPC, P], F32)
+            live["dg", h, c] = dg
+            for r in range(TPC):
+                n = c * TPC + r
+                nc.tensor.matmul(dg[:, r, :], lhsT=ident[:], rhs=mask_b[:, 0, :], start=True, stop=False)
+                nc.tensor.matmul(dg[:, r, :].rearrange("p (u s) -> p u s", u=2), lhsT=qT[:, h, n * P:(n + 1) * P],
+                                 rhs=kT[:, h, :, n * HT:(n + 1) * HT], start=False, stop=True)
+
+        def diagonal_max(h, c):
+            rd = small.tile([P, TPC], F32)
+            live["rd", h, c] = rd
+            nc.vector.tensor_reduce(out=rd[:], in_=live["dg", h, c][:], axis=AX.X, op=ALU.max)
+
+        def older(n):
+            return min(n, TPC)
+
+        def scores_unmasked(x):
+            h, n = tiles[x]
+            if n == 0:
+                return
+            sa = ps_a.tile([P, 2, TPC * HT], F32)
+            live["sa", x] = sa
+            first = TPC - older(n) if n < TPC else 1
+            nc.tensor.matmul(sa[:, :, first * HT:TPC * HT], lhsT=qT[:, h, n * P:(n + 1) * P],
+                             rhs=kT[:, h, :, (n - TPC + first) * HT:n * HT], start=True, stop=True)
+
+        def scores_masked(x):
+            h, n = tiles[x]
+            if n < TPC:
+                return
+            sa = live["sa", x]
+            nc.tensor.matmul(sa[:, :, 0:HT], lhsT=ident[:], rhs=mask_b[:, 1, :].rearrange("p (u s) -> p u s", u=2),
+                             start=True, stop=False)
+            nc.tensor.matmul(sa[:, :, 0:HT], lhsT=qT[:, h, n * P:(n + 1) * P],
+                             rhs=kT[:, h, :, (n - TPC) * HT:(n - TPC + 1) * HT], start=False, stop=True)
+
+        def row_max(x):
+            h, n = tiles[x]
+            if n == 0:
+                return
+            r1 = small.tile([P, 1], F32)
+            live["r1", x] = r1
+            nc.vector.tensor_reduce(out=r1[:], in_=live["sa", x][:, :, (TPC - older(n)) * HT:], axis=AX.XY,
+                                    op=ALU.max)
+
+        def bias(x):
+            h, n = tiles[x]
+            rd = live["rd", h, n // TPC]
+            nb = small.tile([P, 1], F32)
+            live["nb", x] = nb
+            if n == 0:
+                nc.vector.tensor_scalar(out=nb[:], in0=rd[:, 0:1], scalar1=-SCALE, scalar2=None, op0=ALU.mult)
+            else:
+                nc.vector.tensor_scalar(out=nb[:], in0=live["r1", x][:], scalar1=rd[:, n % TPC:n % TPC + 1],
+                                        scalar2=-SCALE, op0=ALU.max, op1=ALU.mult)
+
+        def exponentials(x):
+            h, n = tiles[x]
+            e = e_fix[h * TPC + n % TPC]
+            nb = live["nb", x]
+            dia = (n % TPC + TPC) * HT
+            if n > 0:
+                nc.scalar.activation(out=e[:, :, dia - older(n) * HT:dia],
+                                     in_=live["sa", x][:, :, (TPC - older(n)) * HT:], func=ACT.Exp,
+                                     bias=nb[:], scale=SCALE, accum_out=rs[:, x, 0:1])
+            nc.scalar.activation(out=e[:, :, dia:dia + HT],
+                                 in_=live["dg", h, n // TPC][:, n % TPC, :].rearrange("p (u s) -> p u s", u=2),
+                                 func=ACT.Exp, bias=nb[:], scale=SCALE, accum_out=rs[:, x, 1:2])
+
+        def first_pass(n):
+            return 0 if n >= TPC else 1
+
+        def transpose_e(x):
+            h, n = tiles[x]
+            et = ps_t.tile([P, 2, 2, P], F32, tag="tp")
+            live["et", x] = et
+            words = e_fix[h * TPC + n % TPC][:].rearrange("p u s -> p (u s)").bitcast(F32)
+            for a in range(first_pass(n), 2):
+                for u in range(2):
+                    nc.tensor.transpose(et[:, a, u, :], words[:, (2 * u + a) * P:(2 * u + a + 1) * P], ident_w[:])
+
+        def copy_e(x):
+            h, n = tiles[x]
+            a0 = first_pass(n)
+            ge = gpool.tile([P, 2, P, TPC], BF16, align_bytes=64)
+            live["ge", x] = ge
+            pairs = ge[:].rearrange("p a q t -> p (a q t)").bitcast(F32).rearrange("p (a q u) -> p a q u", a=2, u=2)
+            nc.scalar.copy(out=pairs[:, a0:2], in_=live["et", x][:, a0:2].rearrange("p a u q -> p a q u"))
+
+        def quantise_e(x):
+            h, n = tiles[x]
+            a0 = first_pass(n)
+            cod = cpool.tile([P, 2 * P], U32, align_bytes=64)
+            scl = cpool.tile([P, 2 * P], U8, align_bytes=64)
+            live["cod", x] = cod
+            live["scl", x] = scl
+            nc.vector.quantize_mx(out=cod[:, a0 * P:2 * P].bitcast(FP8X4), scales=scl[:, a0 * P:2 * P],
+                                  in_=live["ge", x][:, a0:2].rearrange("p a q t -> p (a q t)"))
+
+        def e_times_v(x):
+            h, n = tiles[x]
+            a0 = first_pass(n)
+            acc = ps_o.tile([P, D], F32)
+            live["acc", x] = acc
+            cod = live["cod", x]
+            scl = live["scl", x]
+            for a in range(a0, 2):
+                g = n // TPC - 1 + a
+                nc.tensor.matmul_mx(out=acc[:], lhsT=cod[:, a * P:(a + 1) * P].bitcast(FP8X4),
+                                    lhsT_scale=scl[:, a * P:(a + 1) * P],
+                                    rhs=v_cod[:, h, g * D:(g + 1) * D].bitcast(FP8X4),
+                                    rhs_scale=v_scl[:, h, g * D:(g + 1) * D],
+                                    start=(a == a0), stop=(a == 1))
+
+        def add_row_sums(x):
+            rsm = small.tile([P, 2], F32)
+            live["rsm", x] = rsm
+            nc.vector.tensor_reduce(out=rsm[:], in_=rs[:, x:x + 2, :], axis=AX.X, op=ALU.add)
+
+        def invert_row_sums(x):
+            rcp = small.tile([P, 2], F32)
+            live["rcp", x] = rcp
+            nc.vector.reciprocal(rcp[:], live["rsm", x][:])
+
+        def scale_and_store(x):
+            h, n = tiles[x]
+            osb = opool.tile([P, D], F32)
+            rcp = live["rcp", x - x % 2]
+            nc.vector.tensor_scalar(out=osb[:], in0=live["acc", x][:], scalar1=rcp[:, x % 2:x % 2 + 1], scalar2=None,
+                                    op0=ALU.mult)
+            nc.sync.dma_start(out=ov[h][:, n, :], in_=osb[:])
+
+        def stage(work, x, every=1):
+            if 0 <= x < NQ and x % every == 0:
+                work(x)
+
+        transpose_qk(0, 0)
+        copy_qk(0, 0)
+        diagonal_scores(0, 0)
+        for g in range(NCH):
+            regroup_v(0, g)
+        quantise_v(0, 0)
+        diagonal_max(0, 0)
+        quantise_v(0, 1)
+        for s in range(-2, NQ + 4):
+            new_qk = chunks[s // 3 + 1] if s >= 0 and s % 3 == 0 and s // 3 + 1 < H * NCH else None
+            new_dg = chunks[s // TPC + 1] if s >= 0 and s % TPC == 1 and s // TPC + 1 < H * NCH else None
+            stage(transpose_e, s - 1)
+            stage(scores_unmasked, s + 2)
+            stage(e_times_v, s - 3)
+            stage(scores_masked, s + 2)
+            if new_qk:
+                transpose_qk(new_qk[0], new_qk[1])
+            if new_dg:
+                diagonal_scores(new_dg[0], new_dg[1])
+            stage(row_max, s + 1)
+            stage(invert_row_sums, s - 3, 2)
+            stage(quantise_e, s - 2)
+            stage(bias, s + 1)
+            stage(scale_and_store, s - 3)
+            stage(add_row_sums, s - 2, 2)
+            stage(exponentials, s)
+            stage(copy_e, s - 1)
+            if 0 <= s < 2:
+                quantise_v(0, s + 2)
+            if 2 * NCH <= s < 4 * NCH and s % 2 == 0:
+                regroup_v(chunks[s // 2][0], chunks[s // 2][1])
+            if 2 * NCH <= s < 4 * NCH and s % 2 == 1:
+                quantise_v(chunks[s // 2][0], chunks[s // 2][1])
+            if new_qk:
+                copy_qk(new_qk[0], new_qk[1])
+            if new_dg:
+                diagonal_max(new_dg[0], new_dg[1])

@@ -41,7 +41,7 @@ def tile_multiheadattn_kernel(tc, q, k, v, layer_idx, out):
         small = ctx.enter_context(tc.tile_pool(name="small", bufs=10))
         gpool = ctx.enter_context(tc.tile_pool(name="gpool", bufs=3))
         cpool = ctx.enter_context(tc.tile_pool(name="cpool", bufs=3))
-        opool = ctx.enter_context(tc.tile_pool(name="opool", bufs=4))
+        opool = ctx.enter_context(tc.tile_pool(name="opool", bufs=2))
         ps_a = ctx.enter_context(tc.psum_pool(name="ps_a", bufs=3))
         ps_d = ctx.enter_context(tc.psum_pool(name="ps_d", bufs=2))
         ps_t = ctx.enter_context(tc.psum_pool(name="ps_t", bufs=2))
@@ -61,7 +61,7 @@ def tile_multiheadattn_kernel(tc, q, k, v, layer_idx, out):
         mask_f = keep.tile([P, 2, P], F32)
         mask_b = keep.tile([P, 2, P], BF16)
         warm = keep.tile([P, 2], F32)
-        rs = keep.tile([P, NQ, 2], F32)
+        rs = keep.tile([P, H, NT, 2], F32)
         e_fix = []
         for h in range(H):
             for r in range(TPC):
@@ -185,11 +185,12 @@ def tile_multiheadattn_kernel(tc, q, k, v, layer_idx, out):
             rd = live["rd", h, n // TPC]
             nb = small.tile([P, 1], F32)
             live["nb", x] = nb
+            engine = nc.vector if x < TPC else nc.gpsimd
             if n == 0:
-                nc.vector.tensor_scalar(out=nb[:], in0=rd[:, 0:1], scalar1=-SCALE, scalar2=None, op0=ALU.mult)
+                engine.tensor_scalar(out=nb[:], in0=rd[:, 0:1], scalar1=-SCALE, scalar2=None, op0=ALU.mult)
             else:
-                nc.vector.tensor_scalar(out=nb[:], in0=live["r1", x][:], scalar1=rd[:, n % TPC:n % TPC + 1],
-                                        scalar2=-SCALE, op0=ALU.max, op1=ALU.mult)
+                engine.tensor_scalar(out=nb[:], in0=live["r1", x][:], scalar1=rd[:, n % TPC:n % TPC + 1],
+                                     scalar2=-SCALE, op0=ALU.max, op1=ALU.mult)
 
         def exponentials(x):
             h, n = tiles[x]
@@ -199,10 +200,10 @@ def tile_multiheadattn_kernel(tc, q, k, v, layer_idx, out):
             if n > 0:
                 nc.scalar.activation(out=e[:, :, dia - older(n) * HT:dia],
                                      in_=live["sa", x][:, :, (TPC - older(n)) * HT:], func=ACT.Exp,
-                                     bias=nb[:], scale=SCALE, accum_out=rs[:, x, 0:1])
+                                     bias=nb[:], scale=SCALE, accum_out=rs[:, h, n, 0:1])
             nc.scalar.activation(out=e[:, :, dia:dia + HT],
                                  in_=live["dg", h, n // TPC][:, n % TPC, :].rearrange("p (u s) -> p u s", u=2),
-                                 func=ACT.Exp, bias=nb[:], scale=SCALE, accum_out=rs[:, x, 1:2])
+                                 func=ACT.Exp, bias=nb[:], scale=SCALE, accum_out=rs[:, h, n, 1:2])
 
         def first_pass(n):
             return 0 if n >= TPC else 1
@@ -219,53 +220,59 @@ def tile_multiheadattn_kernel(tc, q, k, v, layer_idx, out):
         def copy_e(x):
             h, n = tiles[x]
             a0 = first_pass(n)
-            ge = gpool.tile([P, 2, P, TPC], BF16, align_bytes=64)
-            live["ge", x] = ge
-            pairs = ge[:].rearrange("p a q t -> p (a q t)").bitcast(F32).rearrange("p (a q u) -> p a q u", a=2, u=2)
-            nc.scalar.copy(out=pairs[:, a0:2], in_=live["et", x][:, a0:2].rearrange("p a u q -> p a q u"))
+            if x % 2 == 0:
+                ge = gpool.tile([P, 2, 2, P, TPC], BF16, align_bytes=64)
+                live["ge", x // 2] = ge
+            ge = live["ge", x // 2]
+            pairs = ge[:].rearrange("p a j q t -> p (a j q t)").bitcast(F32)
+            pairs = pairs.rearrange("p (a j q u) -> p a j q u", a=2, j=2, u=2)
+            nc.scalar.copy(out=pairs[:, a0:2, x % 2], in_=live["et", x][:, a0:2].rearrange("p a u q -> p a q u"))
 
         def quantise_e(x):
             h, n = tiles[x]
             a0 = first_pass(n)
-            cod = cpool.tile([P, 2 * P], U32, align_bytes=64)
-            scl = cpool.tile([P, 2 * P], U8, align_bytes=64)
-            live["cod", x] = cod
-            live["scl", x] = scl
-            nc.vector.quantize_mx(out=cod[:, a0 * P:2 * P].bitcast(FP8X4), scales=scl[:, a0 * P:2 * P],
-                                  in_=live["ge", x][:, a0:2].rearrange("p a q t -> p (a q t)"))
+            cod = cpool.tile([P, 4 * P], U32, align_bytes=64)
+            scl = cpool.tile([P, 4 * P], U8, align_bytes=64)
+            live["cod", x // 2] = cod
+            live["scl", x // 2] = scl
+            nc.vector.quantize_mx(out=cod[:, 2 * a0 * P:4 * P].bitcast(FP8X4), scales=scl[:, 2 * a0 * P:4 * P],
+                                  in_=live["ge", x // 2][:, a0:2].rearrange("p a j q t -> p (a j q t)"))
 
         def e_times_v(x):
-            h, n = tiles[x]
-            a0 = first_pass(n)
-            acc = ps_o.tile([P, D], F32)
-            live["acc", x] = acc
-            cod = live["cod", x]
-            scl = live["scl", x]
-            for a in range(a0, 2):
-                g = n // TPC - 1 + a
-                nc.tensor.matmul_mx(out=acc[:], lhsT=cod[:, a * P:(a + 1) * P].bitcast(FP8X4),
-                                    lhsT_scale=scl[:, a * P:(a + 1) * P],
-                                    rhs=v_cod[:, h, g * D:(g + 1) * D].bitcast(FP8X4),
-                                    rhs_scale=v_scl[:, h, g * D:(g + 1) * D],
-                                    start=(a == a0), stop=(a == 1))
+            acc = ps_o.tile([P, TPC, D], F32)
+            live["acc"] = acc
+            for y in range(x, x + TPC):
+                h, n = tiles[y]
+                a0 = first_pass(n)
+                cod = live["cod", y // 2]
+                scl = live["scl", y // 2]
+                for a in range(a0, 2):
+                    g = n // TPC - 1 + a
+                    z = 2 * a + y % 2
+                    nc.tensor.matmul_mx(out=acc[:, n % TPC, :], lhsT=cod[:, z * P:(z + 1) * P].bitcast(FP8X4),
+                                        lhsT_scale=scl[:, z * P:(z + 1) * P],
+                                        rhs=v_cod[:, h, g * D:(g + 1) * D].bitcast(FP8X4),
+                                        rhs_scale=v_scl[:, h, g * D:(g + 1) * D],
+                                        start=(a == a0), stop=(a == 1))
 
         def add_row_sums(x):
-            rsm = small.tile([P, 2], F32)
-            live["rsm", x] = rsm
-            nc.vector.tensor_reduce(out=rsm[:], in_=rs[:, x:x + 2, :], axis=AX.X, op=ALU.add)
+            h, c = chunks[x // TPC]
+            rsm = small.tile([P, TPC], F32)
+            live["rsm"] = rsm
+            nc.gpsimd.tensor_tensor(out=rsm[:], in0=rs[:, h, c * TPC:(c + 1) * TPC, 0],
+                                    in1=rs[:, h, c * TPC:(c + 1) * TPC, 1], op=ALU.add)
 
         def invert_row_sums(x):
-            rcp = small.tile([P, 2], F32)
-            live["rcp", x] = rcp
-            nc.vector.reciprocal(rcp[:], live["rsm", x][:])
+            rcp = small.tile([P, TPC], F32)
+            live["rcp"] = rcp
+            nc.vector.reciprocal(rcp[:], live["rsm"][:])
 
         def scale_and_store(x):
-            h, n = tiles[x]
-            osb = opool.tile([P, D], F32)
-            rcp = live["rcp", x - x % 2]
-            nc.vector.tensor_scalar(out=osb[:], in0=live["acc", x][:], scalar1=rcp[:, x % 2:x % 2 + 1], scalar2=None,
-                                    op0=ALU.mult)
-            nc.sync.dma_start(out=ov[h][:, n, :], in_=osb[:])
+            h, c = chunks[x // TPC]
+            osb = opool.tile([P, TPC, D], F32)
+            nc.vector.tensor_tensor(out=osb[:], in0=live["acc"][:],
+                                    in1=live["rcp"][:].unsqueeze(2).to_broadcast([P, TPC, D]), op=ALU.mult)
+            nc.sync.dma_start(out=ov[h][:, c * TPC:(c + 1) * TPC, :], in_=osb[:])
 
         def stage(work, x, every=1):
             if 0 <= x < NQ and x % every == 0:
@@ -284,18 +291,18 @@ def tile_multiheadattn_kernel(tc, q, k, v, layer_idx, out):
             new_dg = chunks[s // TPC + 1] if s >= 0 and s % TPC == 1 and s // TPC + 1 < H * NCH else None
             stage(transpose_e, s - 1)
             stage(scores_unmasked, s + 2)
-            stage(e_times_v, s - 3)
+            stage(e_times_v, s - 6, TPC)
             stage(scores_masked, s + 2)
             if new_qk:
                 transpose_qk(new_qk[0], new_qk[1])
             if new_dg:
                 diagonal_scores(new_dg[0], new_dg[1])
             stage(row_max, s + 1)
-            stage(invert_row_sums, s - 3, 2)
-            stage(quantise_e, s - 2)
             stage(bias, s + 1)
-            stage(scale_and_store, s - 3)
-            stage(add_row_sums, s - 2, 2)
+            stage(add_row_sums, s - 4, TPC)
+            stage(quantise_e, s - 3, 2)
+            stage(invert_row_sums, s - 5, TPC)
+            stage(scale_and_store, s - 6, TPC)
             stage(exponentials, s)
             stage(copy_e, s - 1)
             if 0 <= s < 2:

@@ -185,12 +185,11 @@ def tile_multiheadattn_kernel(tc, q, k, v, layer_idx, out):
             rd = live["rd", h, n // TPC]
             nb = small.tile([P, 1], F32)
             live["nb", x] = nb
-            engine = nc.vector if x < TPC else nc.gpsimd
             if n == 0:
-                engine.tensor_scalar(out=nb[:], in0=rd[:, 0:1], scalar1=-SCALE, scalar2=None, op0=ALU.mult)
+                nc.vector.tensor_scalar(out=nb[:], in0=rd[:, 0:1], scalar1=-SCALE, scalar2=None, op0=ALU.mult)
             else:
-                engine.tensor_scalar(out=nb[:], in0=live["r1", x][:], scalar1=rd[:, n % TPC:n % TPC + 1],
-                                     scalar2=-SCALE, op0=ALU.max, op1=ALU.mult)
+                nc.vector.tensor_scalar(out=nb[:], in0=live["r1", x][:], scalar1=rd[:, n % TPC:n % TPC + 1],
+                                        scalar2=-SCALE, op0=ALU.max, op1=ALU.mult)
 
         def exponentials(x):
             h, n = tiles[x]
@@ -259,8 +258,7 @@ def tile_multiheadattn_kernel(tc, q, k, v, layer_idx, out):
             h, c = chunks[x // TPC]
             rsm = small.tile([P, TPC], F32)
             live["rsm"] = rsm
-            nc.gpsimd.tensor_tensor(out=rsm[:], in0=rs[:, h, c * TPC:(c + 1) * TPC, 0],
-                                    in1=rs[:, h, c * TPC:(c + 1) * TPC, 1], op=ALU.add)
+            nc.vector.tensor_reduce(out=rsm[:], in_=rs[:, h, c * TPC:(c + 1) * TPC, :], axis=AX.X, op=ALU.add)
 
         def invert_row_sums(x):
             rcp = small.tile([P, TPC], F32)
@@ -298,9 +296,9 @@ def tile_multiheadattn_kernel(tc, q, k, v, layer_idx, out):
             if new_dg:
                 diagonal_scores(new_dg[0], new_dg[1])
             stage(row_max, s + 1)
-            stage(bias, s + 1)
-            stage(add_row_sums, s - 4, TPC)
             stage(quantise_e, s - 3, 2)
+            stage(add_row_sums, s - 4, TPC)
+            stage(bias, s + 1)
             stage(invert_row_sums, s - 5, TPC)
             stage(scale_and_store, s - 6, TPC)
             stage(exponentials, s)

@@ -41,7 +41,7 @@ def tile_multiheadattn_kernel(tc, q, k, v, layer_idx, out):
         small = ctx.enter_context(tc.tile_pool(name="small", bufs=10))
         gpool = ctx.enter_context(tc.tile_pool(name="gpool", bufs=3))
         cpool = ctx.enter_context(tc.tile_pool(name="cpool", bufs=3))
-        opool = ctx.enter_context(tc.tile_pool(name="opool", bufs=2))
+        opool = ctx.enter_context(tc.tile_pool(name="opool", bufs=3))
         ps_a = ctx.enter_context(tc.psum_pool(name="ps_a", bufs=3))
         ps_d = ctx.enter_context(tc.psum_pool(name="ps_d", bufs=2))
         ps_t = ctx.enter_context(tc.psum_pool(name="ps_t", bufs=2))
@@ -134,10 +134,12 @@ def tile_multiheadattn_kernel(tc, q, k, v, layer_idx, out):
                                   scales=v_scl[:, h, g * D:(g + 1) * D],
                                   in_=v_grp[:, h, g].rearrange("p d t -> p (d t)"))
 
-        def diagonal_scores(h, c):
-            dg = ps_d.tile([P, TPC, P], F32)
-            live["dg", h, c] = dg
-            for r in range(TPC):
+        def diagonal_scores(h, c, r0):
+            if r0 == 0:
+                dg = ps_d.tile([P, TPC, P], F32)
+                live["dg", h, c] = dg
+            dg = live["dg", h, c]
+            for r in range(r0, r0 + 2):
                 n = c * TPC + r
                 nc.tensor.matmul(dg[:, r, :], lhsT=ident[:], rhs=mask_b[:, 0, :], start=True, stop=False)
                 nc.tensor.matmul(dg[:, r, :].rearrange("p (u s) -> p u s", u=2), lhsT=qT[:, h, n * P:(n + 1) * P],
@@ -238,9 +240,9 @@ def tile_multiheadattn_kernel(tc, q, k, v, layer_idx, out):
                                   in_=live["ge", x // 2][:, a0:2].rearrange("p a j q t -> p (a j q t)"))
 
         def e_times_v(x):
-            acc = ps_o.tile([P, TPC, D], F32)
-            live["acc"] = acc
-            for y in range(x, x + TPC):
+            acc = ps_o.tile([P, 2, D], F32)
+            live["acc", x] = acc
+            for y in range(x, x + 2):
                 h, n = tiles[y]
                 a0 = first_pass(n)
                 cod = live["cod", y // 2]
@@ -248,29 +250,33 @@ def tile_multiheadattn_kernel(tc, q, k, v, layer_idx, out):
                 for a in range(a0, 2):
                     g = n // TPC - 1 + a
                     z = 2 * a + y % 2
-                    nc.tensor.matmul_mx(out=acc[:, n % TPC, :], lhsT=cod[:, z * P:(z + 1) * P].bitcast(FP8X4),
+                    nc.tensor.matmul_mx(out=acc[:, n % 2, :], lhsT=cod[:, z * P:(z + 1) * P].bitcast(FP8X4),
                                         lhsT_scale=scl[:, z * P:(z + 1) * P],
                                         rhs=v_cod[:, h, g * D:(g + 1) * D].bitcast(FP8X4),
                                         rhs_scale=v_scl[:, h, g * D:(g + 1) * D],
                                         start=(a == a0), stop=(a == 1))
 
+        def first_of_two(x):
+            h, n = tiles[x]
+            return h, n - n % 2
+
         def add_row_sums(x):
-            h, c = chunks[x // TPC]
-            rsm = small.tile([P, TPC], F32)
-            live["rsm"] = rsm
-            nc.vector.tensor_reduce(out=rsm[:], in_=rs[:, h, c * TPC:(c + 1) * TPC, :], axis=AX.X, op=ALU.add)
+            h, n = first_of_two(x)
+            rsm = small.tile([P, 2], F32)
+            live["rsm", x] = rsm
+            nc.gpsimd.tensor_tensor(out=rsm[:], in0=rs[:, h, n:n + 2, 0], in1=rs[:, h, n:n + 2, 1], op=ALU.add)
 
         def invert_row_sums(x):
-            rcp = small.tile([P, TPC], F32)
-            live["rcp"] = rcp
-            nc.vector.reciprocal(rcp[:], live["rsm"][:])
+            rcp = small.tile([P, 2], F32)
+            live["rcp", x] = rcp
+            nc.vector.reciprocal(rcp[:], live["rsm", x][:])
 
         def scale_and_store(x):
-            h, c = chunks[x // TPC]
-            osb = opool.tile([P, TPC, D], F32)
-            nc.vector.tensor_tensor(out=osb[:], in0=live["acc"][:],
-                                    in1=live["rcp"][:].unsqueeze(2).to_broadcast([P, TPC, D]), op=ALU.mult)
-            nc.sync.dma_start(out=ov[h][:, c * TPC:(c + 1) * TPC, :], in_=osb[:])
+            h, n = first_of_two(x)
+            osb = opool.tile([P, 2, D], F32)
+            nc.vector.tensor_tensor(out=osb[:], in0=live["acc", x][:],
+                                    in1=live["rcp", x][:].unsqueeze(2).to_broadcast([P, 2, D]), op=ALU.mult)
+            nc.sync.dma_start(out=ov[h][:, n:n + 2, :], in_=osb[:])
 
         def stage(work, x, every=1):
             if 0 <= x < NQ and x % every == 0:
@@ -278,29 +284,34 @@ def tile_multiheadattn_kernel(tc, q, k, v, layer_idx, out):
 
         transpose_qk(0, 0)
         copy_qk(0, 0)
-        diagonal_scores(0, 0)
+        diagonal_scores(0, 0, 0)
+        diagonal_scores(0, 0, 2)
         for g in range(NCH):
             regroup_v(0, g)
         quantise_v(0, 0)
         diagonal_max(0, 0)
         quantise_v(0, 1)
-        for s in range(-2, NQ + 4):
+        for s in range(-2, NQ + 5):
             new_qk = chunks[s // 3 + 1] if s >= 0 and s % 3 == 0 and s // 3 + 1 < H * NCH else None
-            new_dg = chunks[s // TPC + 1] if s >= 0 and s % TPC == 1 and s // TPC + 1 < H * NCH else None
+            new_dg = []
+            if s > 0 and s % 2 == 0 and s // TPC + 1 < H * NCH:
+                new_dg = [s % TPC] if s >= TPC else [0, 2] if s == 2 else []
             stage(transpose_e, s - 1)
             stage(scores_unmasked, s + 2)
-            stage(e_times_v, s - 6, TPC)
+            stage(e_times_v, s - 5, 2)
             stage(scores_masked, s + 2)
             if new_qk:
                 transpose_qk(new_qk[0], new_qk[1])
-            if new_dg:
-                diagonal_scores(new_dg[0], new_dg[1])
+            for r0 in new_dg:
+                diagonal_scores(chunks[s // TPC + 1][0], chunks[s // TPC + 1][1], r0)
+            if s >= 0 and s % TPC == 3 and s // TPC + 1 < H * NCH:
+                diagonal_max(chunks[s // TPC + 1][0], chunks[s // TPC + 1][1])
             stage(row_max, s + 1)
             stage(quantise_e, s - 3, 2)
-            stage(add_row_sums, s - 4, TPC)
             stage(bias, s + 1)
-            stage(invert_row_sums, s - 5, TPC)
-            stage(scale_and_store, s - 6, TPC)
+            stage(invert_row_sums, s - 4, 2)
+            stage(scale_and_store, s - 5, 2)
+            stage(add_row_sums, s - 3, 2)
             stage(exponentials, s)
             stage(copy_e, s - 1)
             if 0 <= s < 2:
@@ -311,5 +322,3 @@ def tile_multiheadattn_kernel(tc, q, k, v, layer_idx, out):
                 quantise_v(chunks[s // 2][0], chunks[s // 2][1])
             if new_qk:
                 copy_qk(new_qk[0], new_qk[1])
-            if new_dg:
-                diagonal_max(new_dg[0], new_dg[1])

@@ -6,6 +6,7 @@ from concourse.masks import make_identity
 
 F32 = mybir.dt.float32
 BF16 = mybir.dt.bfloat16
+I32 = mybir.dt.int32
 U32 = mybir.dt.uint32
 U8 = mybir.dt.uint8
 FP8X4 = mybir.dt.float8_e4m3fn_x4
@@ -18,10 +19,13 @@ P = 128
 HT = P // 2
 NT = S // P
 TPC = W // P
+QP = P // TPC
 NCH = S // W
 NQ = H * NT
+NC = H * NCH
 SCALE = 1.0 / math.sqrt(D)
 MASKED = -17179869184.0
+ROW = D + D // 4
 FLOPS = 2 * 2 * H * D * (W * W + (NCH - 1) * W * 2 * W)
 
 
@@ -38,12 +42,13 @@ def tile_multiheadattn_kernel(tc, q, k, v, layer_idx, out):
 
     with ExitStack() as ctx:
         keep = ctx.enter_context(tc.tile_pool(name="keep", bufs=1))
-        small = ctx.enter_context(tc.tile_pool(name="small", bufs=10))
+        small = ctx.enter_context(tc.tile_pool(name="small", bufs=12))
+        epool = ctx.enter_context(tc.tile_pool(name="epool", bufs=4))
         gpool = ctx.enter_context(tc.tile_pool(name="gpool", bufs=3))
-        cpool = ctx.enter_context(tc.tile_pool(name="cpool", bufs=3))
-        opool = ctx.enter_context(tc.tile_pool(name="opool", bufs=3))
+        cpool = ctx.enter_context(tc.tile_pool(name="cpool", bufs=5))
+        opool = ctx.enter_context(tc.tile_pool(name="opool", bufs=6))
         ps_a = ctx.enter_context(tc.psum_pool(name="ps_a", bufs=3))
-        ps_d = ctx.enter_context(tc.psum_pool(name="ps_d", bufs=2))
+        ps_b = ctx.enter_context(tc.psum_pool(name="ps_b", bufs=2))
         ps_t = ctx.enter_context(tc.psum_pool(name="ps_t", bufs=2))
         ps_o = ctx.enter_context(tc.psum_pool(name="ps_o", bufs=1))
         ctx.enter_context(tc.manual_schedule())
@@ -54,19 +59,20 @@ def tile_multiheadattn_kernel(tc, q, k, v, layer_idx, out):
         qT = keep.tile([P, H, S], BF16)
         kT = keep.tile([P, H, 2, S // 2], BF16)
         v_grp = keep.tile([P, H, NCH, D, TPC], BF16, align_bytes=64)
-        v_cod = keep.tile([P, H, NCH * D], U32, align_bytes=64)
-        v_scl = keep.tile([P, H, NCH * D], U8, align_bytes=64)
+        v_qnt = keep.tile([P, H, NCH, ROW], U32, align_bytes=64)
+        v_win = keep.tile([P, H, TPC - 1, NCH - 1, ROW], U32, align_bytes=64)
+        v_far = keep.tile([P, H, NCH - 1, TPC, D], U32, align_bytes=64)
         ident = keep.tile([P, P], BF16)
         ident_w = keep.tile([P, P], F32)
         mask_f = keep.tile([P, 2, P], F32)
         mask_b = keep.tile([P, 2, P], BF16)
         warm = keep.tile([P, 2], F32)
+        zeros = keep.tile([P, W], BF16)
         rs = keep.tile([P, H, NT, 2], F32)
-        e_fix = []
-        for h in range(H):
-            for r in range(TPC):
-                e_hr = keep.tile([P, 2, W], BF16, name="e%d%d" % (h, r))
-                e_fix.append(e_hr)
+        e_first = []
+        for r in range(TPC):
+            e_r = keep.tile([P, 2, TPC * HT], BF16, name="e%d" % r)
+            e_first.append(e_r)
 
         def load(queue, raw, view, h, c):
             queue.dma_start(out=raw[:, h, c * TPC:(c + 1) * TPC, :], in_=view[h][:, c * TPC:(c + 1) * TPC, :])
@@ -83,7 +89,7 @@ def tile_multiheadattn_kernel(tc, q, k, v, layer_idx, out):
                 nc.sync.dma_start(out=v_raw[:, 1], in_=vv[1])
 
         make_identity(nc, ident[:])
-        make_identity(nc, ident_w[:])
+        nc.vector.memset(zeros[:], 0.0)
         nc.vector.memset(warm[:, 0:1], 0.0)
         nc.scalar.activation(out=warm[:, 1:2], in_=warm[:, 0:1], func=ACT.Exp)
         nc.gpsimd.memset(mask_f[:], 0.0)
@@ -91,14 +97,12 @@ def tile_multiheadattn_kernel(tc, q, k, v, layer_idx, out):
                                 base=0, pattern=[[-1, P]], channel_multiplier=1)
         nc.gpsimd.affine_select(out=mask_f[:, 1, :], in_=mask_f[:, 1, :], compare_op=ALU.is_ge, fill=MASKED,
                                 base=-1, pattern=[[1, P]], channel_multiplier=-1)
-        for h in range(H):
-            for r in range(TPC):
-                e_hr = e_fix[h * TPC + r]
-                if r > 0:
-                    nc.gpsimd.memset(e_hr[:, :, 0:HT * r], 0.0)
-                if r < TPC - 1:
-                    nc.gpsimd.memset(e_hr[:, :, HT * (r + TPC + 1):W], 0.0)
+        make_identity(nc, ident_w[:])
+        for r in range(TPC - 1):
+            nc.gpsimd.memset(e_first[r][:, :, HT * (r + 1):], 0.0)
+        nc.gpsimd.memset(v_far[:], 0)
         nc.vector.memset(rs[:], 0.0)
+        nc.vector.memset(v_qnt[:, :, :, D:ROW].bitcast(I32), 0)
         for y in range(2):
             nc.vector.tensor_copy(out=mask_b[:, y, :].rearrange("p (u w i) -> p u w i", u=2, i=2),
                                   in_=mask_f[:, y, :].rearrange("p (w u i) -> p u w i", u=2, i=2))
@@ -115,146 +119,168 @@ def tile_multiheadattn_kernel(tc, q, k, v, layer_idx, out):
 
         def copy_qk(h, c):
             tp = live["tp", h, c]
-            nc.vector.tensor_copy(out=qT[:, h, c * W:(c + 1) * W], in_=tp[:, 0:TPC, :].rearrange("p j s -> p (j s)"))
+            queries = tp[:, 0:TPC, :].rearrange("p j s -> p (j s)")
             keys = tp[:, TPC:2 * TPC, :].rearrange("p j s -> p (j s)")
-            nc.vector.tensor_copy(
-                out=kT[:, h, :, c * TPC * HT:(c + 1) * TPC * HT].rearrange("p u (w i) -> p u w i", i=2),
-                in_=keys.rearrange("p (w u i) -> p u w i", u=2, i=2))
+            i = chunks.index((h, c))
+            copy_q = nc.scalar.copy if 1 <= i <= NCH else nc.vector.tensor_copy
+            copy_k = nc.scalar.copy if i == 1 else nc.vector.tensor_copy
+            copy_q(out=qT[:, h, c * W:(c + 1) * W], in_=queries)
+            copy_k(out=kT[:, h, :, c * TPC * HT:(c + 1) * TPC * HT].rearrange("p u (w i) -> p u w i", i=2),
+                   in_=keys.rearrange("p (w u i) -> p u w i", u=2, i=2))
 
         def regroup_v(h, g):
-            dst = v_grp[:, h, g].rearrange("p (c i) t -> p c t i", i=4)
-            src = v_raw[:, h, g].rearrange("p t (c i) -> p c t i", i=4)
-            if h == 0:
-                nc.scalar.copy(out=dst, in_=src)
-            else:
-                nc.vector.tensor_copy(out=dst, in_=src)
+            nc.scalar.copy(out=v_grp[:, h, g].rearrange("p (c i) t -> p c t i", i=4),
+                           in_=v_raw[:, h, g].rearrange("p t (c i) -> p c t i", i=4))
+
+        def words(row):
+            return row[:, 0:D].bitcast(FP8X4)
+
+        def scales(row):
+            return row[:, D:ROW].bitcast(U8)
 
         def quantise_v(h, g):
-            nc.vector.quantize_mx(out=v_cod[:, h, g * D:(g + 1) * D].bitcast(FP8X4),
-                                  scales=v_scl[:, h, g * D:(g + 1) * D],
+            nc.vector.quantize_mx(out=words(v_qnt[:, h, g]), scales=scales(v_qnt[:, h, g]),
                                   in_=v_grp[:, h, g].rearrange("p d t -> p (d t)"))
 
-        def diagonal_scores(h, c, r0):
+        def move_v(h):
+            for r in range(TPC - 1):
+                own = QP * (r + 1)
+                nc.sync.dma_start(out=v_win[0:own, h, r].bitcast(I32), in_=v_qnt[0:own, h, 1:NCH].bitcast(I32))
+                nc.sync.dma_start(out=v_win[own:P, h, r].bitcast(I32), in_=v_qnt[own:P, h, 0:NCH - 1].bitcast(I32))
+            for r in range(TPC):
+                nc.sync.dma_start(out=v_far[QP * r:QP * (r + 1), h, :, r, :].bitcast(I32),
+                                  in_=v_qnt[QP * r:QP * (r + 1), h, 0:NCH - 1, 0:D].bitcast(I32))
+
+        def back_scores(i, r0):
+            h, c = chunks[i]
             if r0 == 0:
-                dg = ps_d.tile([P, TPC, P], F32)
-                live["dg", h, c] = dg
-            dg = live["dg", h, c]
+                sb = ps_b.tile([P, TPC, P], F32)
+                live["sb", i] = sb
+            sb = live["sb", i]
             for r in range(r0, r0 + 2):
                 n = c * TPC + r
-                nc.tensor.matmul(dg[:, r, :], lhsT=ident[:], rhs=mask_b[:, 0, :], start=True, stop=False)
-                nc.tensor.matmul(dg[:, r, :].rearrange("p (u s) -> p u s", u=2), lhsT=qT[:, h, n * P:(n + 1) * P],
-                                 rhs=kT[:, h, :, n * HT:(n + 1) * HT], start=False, stop=True)
+                nc.tensor.matmul(sb[:, r, :], lhsT=ident[:], rhs=mask_b[:, 1, :], start=True, stop=False)
+                nc.tensor.matmul(sb[:, r, :].rearrange("p (u s) -> p u s", u=2), lhsT=qT[:, h, n * P:(n + 1) * P],
+                                 rhs=kT[:, h, :, (n - TPC) * HT:(n - TPC + 1) * HT], start=False, stop=True)
 
-        def diagonal_max(h, c):
-            rd = small.tile([P, TPC], F32)
-            live["rd", h, c] = rd
-            nc.vector.tensor_reduce(out=rd[:], in_=live["dg", h, c][:], axis=AX.X, op=ALU.max)
+        def back_max(i):
+            rb = small.tile([P, TPC], F32)
+            live["rb", i] = rb
+            nc.vector.tensor_reduce(out=rb[:], in_=live["sb", i][:], axis=AX.X, op=ALU.max)
 
-        def older(n):
-            return min(n, TPC)
-
-        def scores_unmasked(x):
+        def near_scores(x):
             h, n = tiles[x]
-            if n == 0:
-                return
+            c, r = n // TPC, n % TPC
             sa = ps_a.tile([P, 2, TPC * HT], F32)
             live["sa", x] = sa
-            first = TPC - older(n) if n < TPC else 1
-            nc.tensor.matmul(sa[:, :, first * HT:TPC * HT], lhsT=qT[:, h, n * P:(n + 1) * P],
-                             rhs=kT[:, h, :, (n - TPC + first) * HT:n * HT], start=True, stop=True)
-
-        def scores_masked(x):
-            h, n = tiles[x]
-            if n < TPC:
-                return
-            sa = live["sa", x]
-            nc.tensor.matmul(sa[:, :, 0:HT], lhsT=ident[:], rhs=mask_b[:, 1, :].rearrange("p (u s) -> p u s", u=2),
+            rows = qT[:, h, n * P:(n + 1) * P]
+            if c > 0 and r < TPC - 1:
+                nc.tensor.matmul(sa[:, :, (r + 1) * HT:], lhsT=rows, rhs=kT[:, h, :, (n - TPC + 1) * HT:c * TPC * HT],
+                                 start=True, stop=True)
+            nc.tensor.matmul(sa[:, :, 0:(r + 1) * HT], lhsT=rows, rhs=kT[:, h, :, c * TPC * HT:(n + 1) * HT],
                              start=True, stop=False)
-            nc.tensor.matmul(sa[:, :, 0:HT], lhsT=qT[:, h, n * P:(n + 1) * P],
-                             rhs=kT[:, h, :, (n - TPC) * HT:(n - TPC + 1) * HT], start=False, stop=True)
+            nc.tensor.matmul(sa[:, :, r * HT:(r + 1) * HT], lhsT=ident[:],
+                             rhs=mask_b[:, 0, :].rearrange("p (u s) -> p u s", u=2), start=False, stop=True)
 
-        def row_max(x):
+        def columns(n):
+            return TPC * HT if n >= TPC else (n + 1) * HT
+
+        def near_max(x):
             h, n = tiles[x]
-            if n == 0:
-                return
-            r1 = small.tile([P, 1], F32)
-            live["r1", x] = r1
-            nc.vector.tensor_reduce(out=r1[:], in_=live["sa", x][:, :, (TPC - older(n)) * HT:], axis=AX.XY,
-                                    op=ALU.max)
+            ra = small.tile([P, 1], F32)
+            live["ra", x] = ra
+            nc.vector.tensor_reduce(out=ra[:], in_=live["sa", x][:, :, 0:columns(n)], axis=AX.XY, op=ALU.max)
 
         def bias(x):
             h, n = tiles[x]
-            rd = live["rd", h, n // TPC]
             nb = small.tile([P, 1], F32)
             live["nb", x] = nb
-            if n == 0:
-                nc.vector.tensor_scalar(out=nb[:], in0=rd[:, 0:1], scalar1=-SCALE, scalar2=None, op0=ALU.mult)
+            if n < TPC:
+                nc.vector.tensor_scalar(out=nb[:], in0=live["ra", x][:], scalar1=-SCALE, scalar2=None, op0=ALU.mult)
             else:
-                nc.vector.tensor_scalar(out=nb[:], in0=live["r1", x][:], scalar1=rd[:, n % TPC:n % TPC + 1],
+                rb = live["rb", x // TPC]
+                nc.vector.tensor_scalar(out=nb[:], in0=live["ra", x][:], scalar1=rb[:, n % TPC:n % TPC + 1],
                                         scalar2=-SCALE, op0=ALU.max, op1=ALU.mult)
 
         def exponentials(x):
             h, n = tiles[x]
-            e = e_fix[h * TPC + n % TPC]
+            r = n % TPC
             nb = live["nb", x]
-            dia = (n % TPC + TPC) * HT
-            if n > 0:
-                nc.scalar.activation(out=e[:, :, dia - older(n) * HT:dia],
-                                     in_=live["sa", x][:, :, (TPC - older(n)) * HT:], func=ACT.Exp,
-                                     bias=nb[:], scale=SCALE, accum_out=rs[:, h, n, 0:1])
-            nc.scalar.activation(out=e[:, :, dia:dia + HT],
-                                 in_=live["dg", h, n // TPC][:, n % TPC, :].rearrange("p (u s) -> p u s", u=2),
-                                 func=ACT.Exp, bias=nb[:], scale=SCALE, accum_out=rs[:, h, n, 1:2])
+            if n < TPC:
+                e = e_first[n]
+            else:
+                e = epool.tile([P, 2, TPC * HT], BF16)
+            live["e", x] = e
+            nc.scalar.activation(out=e[:, :, 0:columns(n)], in_=live["sa", x][:, :, 0:columns(n)], func=ACT.Exp,
+                                 bias=nb[:], scale=SCALE, accum_out=rs[:, h, n, 0:1])
+            if n >= TPC:
+                if x % TPC == 0:
+                    eb = epool.tile([P, 2, TPC * HT], BF16)
+                    live["eb", x // TPC] = eb
+                eb = live["eb", x // TPC]
+                nc.scalar.activation(out=eb[:, :, r * HT:(r + 1) * HT],
+                                     in_=live["sb", x // TPC][:, r, :].rearrange("p (u s) -> p u s", u=2),
+                                     func=ACT.Exp, bias=nb[:], scale=SCALE, accum_out=rs[:, h, n, 1:2])
 
-        def first_pass(n):
-            return 0 if n >= TPC else 1
+        def transpose_words(out_, e):
+            pairs = e[:].rearrange("p u s -> p (u s)").bitcast(F32)
+            for u in range(2):
+                nc.tensor.transpose(out_[:, u, :], pairs[:, u * P:(u + 1) * P], ident_w[:])
 
         def transpose_e(x):
-            h, n = tiles[x]
             et = ps_t.tile([P, 2, 2, P], F32, tag="tp")
             live["et", x] = et
-            words = e_fix[h * TPC + n % TPC][:].rearrange("p u s -> p (u s)").bitcast(F32)
-            for a in range(first_pass(n), 2):
-                for u in range(2):
-                    nc.tensor.transpose(et[:, a, u, :], words[:, (2 * u + a) * P:(2 * u + a + 1) * P], ident_w[:])
+            for j in range(2):
+                transpose_words(et[:, j], live["e", x + j])
+
+        def transpose_back(i):
+            et = ps_t.tile([P, 2, P], F32, tag="tp")
+            live["etb", i] = et
+            transpose_words(et, live["eb", i])
 
         def copy_e(x):
-            h, n = tiles[x]
-            a0 = first_pass(n)
-            if x % 2 == 0:
-                ge = gpool.tile([P, 2, 2, P, TPC], BF16, align_bytes=64)
-                live["ge", x // 2] = ge
-            ge = live["ge", x // 2]
-            pairs = ge[:].rearrange("p a j q t -> p (a j q t)").bitcast(F32)
-            pairs = pairs.rearrange("p (a j q u) -> p a j q u", a=2, j=2, u=2)
-            nc.scalar.copy(out=pairs[:, a0:2, x % 2], in_=live["et", x][:, a0:2].rearrange("p a u q -> p a q u"))
+            ge = gpool.tile([P, 2, P, TPC], BF16, align_bytes=64)
+            live["ge", x] = ge
+            pairs = ge[:].rearrange("p j q t -> p (j q t)").bitcast(F32).rearrange("p (j q u) -> p j q u", j=2, u=2)
+            nc.scalar.copy(out=pairs, in_=live["et", x][:].rearrange("p j u q -> p j q u"))
+
+        def copy_back(i):
+            geb = gpool.tile([P, P, TPC], BF16, align_bytes=64)
+            live["geb", i] = geb
+            pairs = geb[:].rearrange("p q t -> p (q t)").bitcast(F32).rearrange("p (q u) -> p q u", u=2)
+            nc.scalar.copy(out=pairs, in_=live["etb", i][:].rearrange("p u q -> p q u"))
 
         def quantise_e(x):
-            h, n = tiles[x]
-            a0 = first_pass(n)
-            cod = cpool.tile([P, 4 * P], U32, align_bytes=64)
-            scl = cpool.tile([P, 4 * P], U8, align_bytes=64)
-            live["cod", x // 2] = cod
-            live["scl", x // 2] = scl
-            nc.vector.quantize_mx(out=cod[:, 2 * a0 * P:4 * P].bitcast(FP8X4), scales=scl[:, 2 * a0 * P:4 * P],
-                                  in_=live["ge", x // 2][:, a0:2].rearrange("p a j q t -> p (a j q t)"))
+            cod = cpool.tile([P, 2 * P], U32, align_bytes=64)
+            scl = cpool.tile([P, 2 * P], U8, align_bytes=64)
+            live["cod", x] = cod
+            live["scl", x] = scl
+            nc.vector.quantize_mx(out=cod[:].bitcast(FP8X4), scales=scl[:],
+                                  in_=live["ge", x][:].rearrange("p j q t -> p (j q t)"))
+
+        def quantise_back(i):
+            codb = cpool.tile([P, P], U32, align_bytes=64)
+            sclb = cpool.tile([P, P], U8, align_bytes=64)
+            live["codb", i] = codb
+            live["sclb", i] = sclb
+            nc.vector.quantize_mx(out=codb[:].bitcast(FP8X4), scales=sclb[:],
+                                  in_=live["geb", i][:].rearrange("p q t -> p (q t)"))
 
         def e_times_v(x):
-            acc = ps_o.tile([P, 2, D], F32)
+            acc = ps_o.tile([P, 2, D], F32, tag="acc")
             live["acc", x] = acc
-            for y in range(x, x + 2):
-                h, n = tiles[y]
-                a0 = first_pass(n)
-                cod = live["cod", y // 2]
-                scl = live["scl", y // 2]
-                for a in range(a0, 2):
-                    g = n // TPC - 1 + a
-                    z = 2 * a + y % 2
-                    nc.tensor.matmul_mx(out=acc[:, n % 2, :], lhsT=cod[:, z * P:(z + 1) * P].bitcast(FP8X4),
-                                        lhsT_scale=scl[:, z * P:(z + 1) * P],
-                                        rhs=v_cod[:, h, g * D:(g + 1) * D].bitcast(FP8X4),
-                                        rhs_scale=v_scl[:, h, g * D:(g + 1) * D],
-                                        start=(a == a0), stop=(a == 1))
+            for j in range(2):
+                h, n = tiles[x + j]
+                c, r = n // TPC, n % TPC
+                row = v_qnt[:, h, c] if c == 0 or r == TPC - 1 else v_win[:, h, r, c - 1]
+                nc.tensor.matmul_mx(out=acc[:, n % 2, :], lhsT=live["cod", x][:, j * P:(j + 1) * P].bitcast(FP8X4),
+                                    lhsT_scale=live["scl", x][:, j * P:(j + 1) * P],
+                                    rhs=words(row), rhs_scale=scales(row), start=True, stop=c == 0)
+                if c > 0:
+                    i = x // TPC
+                    nc.tensor.matmul_mx(out=acc[:, n % 2, :], lhsT=live["codb", i][:].bitcast(FP8X4),
+                                        lhsT_scale=live["sclb", i][:], rhs=v_far[:, h, c - 1, r].bitcast(FP8X4),
+                                        rhs_scale=scales(v_qnt[:, h, c - 1]), start=False, stop=True)
 
         def first_of_two(x):
             h, n = tiles[x]
@@ -278,47 +304,88 @@ def tile_multiheadattn_kernel(tc, q, k, v, layer_idx, out):
                                     in1=live["rcp", x][:].unsqueeze(2).to_broadcast([P, 2, D]), op=ALU.mult)
             nc.sync.dma_start(out=ov[h][:, n:n + 2, :], in_=osb[:])
 
-        def stage(work, x, every=1):
-            if 0 <= x < NQ and x % every == 0:
-                work(x)
+        def has_back(i):
+            return 0 <= i < NC and chunks[i][1] > 0
 
+        mx_at = {}
+        for x in range(0, NQ, 2):
+            step = x + 5 if not has_back(x // TPC) else x // TPC * TPC + 7 + x % TPC
+            while step in mx_at:
+                step += 1
+            mx_at[step] = x
+        qk_at = {}
+        step = TPC * NC
+        for i in range(NC - 1, 0, -1):
+            needed = TPC * i - TPC if i <= NCH else TPC * i - 2 * TPC
+            step = max(min(needed - 3, step - 2), -1)
+            qk_at[step] = i
+
+        idle = ps_o.tile([P, W], F32, tag="acc")
+
+        def keep_warm(count):
+            for y in range(count):
+                nc.tensor.matmul(idle[:], lhsT=zeros[:, 0:P], rhs=zeros[:], start=True, stop=True)
+
+        keep_warm(4)
         transpose_qk(0, 0)
+        keep_warm(3)
         copy_qk(0, 0)
-        diagonal_scores(0, 0, 0)
-        diagonal_scores(0, 0, 2)
         for g in range(NCH):
             regroup_v(0, g)
-        quantise_v(0, 0)
-        diagonal_max(0, 0)
-        quantise_v(0, 1)
-        for s in range(-2, NQ + 5):
-            new_qk = chunks[s // 3 + 1] if s >= 0 and s % 3 == 0 and s // 3 + 1 < H * NCH else None
-            new_dg = []
-            if s > 0 and s % 2 == 0 and s // TPC + 1 < H * NCH:
-                new_dg = [s % TPC] if s >= TPC else [0, 2] if s == 2 else []
-            stage(transpose_e, s - 1)
-            stage(scores_unmasked, s + 2)
-            stage(e_times_v, s - 5, 2)
-            stage(scores_masked, s + 2)
-            if new_qk:
-                transpose_qk(new_qk[0], new_qk[1])
-            for r0 in new_dg:
-                diagonal_scores(chunks[s // TPC + 1][0], chunks[s // TPC + 1][1], r0)
-            if s >= 0 and s % TPC == 3 and s // TPC + 1 < H * NCH:
-                diagonal_max(chunks[s // TPC + 1][0], chunks[s // TPC + 1][1])
-            stage(row_max, s + 1)
-            stage(quantise_e, s - 3, 2)
-            stage(bias, s + 1)
-            stage(invert_row_sums, s - 4, 2)
-            stage(scale_and_store, s - 5, 2)
-            stage(add_row_sums, s - 3, 2)
-            stage(exponentials, s)
-            stage(copy_e, s - 1)
+        for s in range(-2, max(mx_at) + 2):
+            odd = s % 2 == 1
+            if 2 <= s <= NQ and not odd:
+                transpose_e(s - 2)
+            if s >= TPC and s % TPC == 0 and has_back(s // TPC - 1):
+                transpose_back(s // TPC - 1)
+            if s in mx_at:
+                e_times_v(mx_at[s])
+            if 0 <= s + 2 < NQ:
+                near_scores(s + 2)
+            if s >= 2 and not odd and has_back((s + TPC) // TPC):
+                if s >= TPC:
+                    back_scores((s + TPC) // TPC, s % TPC)
+                else:
+                    back_scores(1, 0)
+                    back_scores(1, 2)
+            if s in qk_at:
+                transpose_qk(*chunks[qk_at[s]])
+            if s % TPC == TPC - 1 and has_back((s + 1) // TPC):
+                back_max((s + 1) // TPC)
+            if 0 <= s + 1 < NQ:
+                near_max(s + 1)
+            if s > 0 and s - 1 in qk_at:
+                copy_qk(*chunks[qk_at[s - 1]])
+            if s - 1 in mx_at:
+                scale_and_store(mx_at[s - 1])
+            if 3 <= s <= NQ + 1 and odd:
+                quantise_e(s - 3)
+            if s >= TPC + 1 and s % TPC == 1 and has_back(s // TPC - 1):
+                quantise_back(s // TPC - 1)
+            if 0 <= s + 1 < NQ:
+                bias(s + 1)
+            if s + 1 in mx_at:
+                invert_row_sums(mx_at[s + 1])
+            if s + 2 in mx_at:
+                add_row_sums(mx_at[s + 2])
+            if 0 <= s < NQ:
+                exponentials(s)
+            if s == 0:
+                copy_qk(*chunks[1])
+            if 2 <= s <= NQ and not odd:
+                copy_e(s - 2)
+            if s >= TPC and s % TPC == 0 and has_back(s // TPC - 1):
+                copy_back(s // TPC - 1)
             if 0 <= s < 2:
-                quantise_v(0, s + 2)
-            if 2 * NCH <= s < 4 * NCH and s % 2 == 0:
-                regroup_v(chunks[s // 2][0], chunks[s // 2][1])
-            if 2 * NCH <= s < 4 * NCH and s % 2 == 1:
-                quantise_v(chunks[s // 2][0], chunks[s // 2][1])
-            if new_qk:
-                copy_qk(new_qk[0], new_qk[1])
+                quantise_v(0, 2 * s)
+                quantise_v(0, 2 * s + 1)
+                if s == 1:
+                    move_v(0)
+            if 3 * NCH <= s < 5 * NCH:
+                g = NCH - 1 - (s - 3 * NCH) // 2
+                if not odd:
+                    regroup_v(1, g)
+                else:
+                    quantise_v(1, g)
+                if s == 5 * NCH - 1:
+                    move_v(1)

@@ -122,15 +122,19 @@ def tile_multiheadattn_kernel(tc, q, k, v, layer_idx, out):
             queries = tp[:, 0:TPC, :].rearrange("p j s -> p (j s)")
             keys = tp[:, TPC:2 * TPC, :].rearrange("p j s -> p (j s)")
             i = chunks.index((h, c))
-            copy_q = nc.scalar.copy if 1 <= i <= NCH else nc.vector.tensor_copy
+            copy_q = nc.scalar.copy if i > 0 else nc.vector.tensor_copy
             copy_k = nc.scalar.copy if i == 1 else nc.vector.tensor_copy
             copy_q(out=qT[:, h, c * W:(c + 1) * W], in_=queries)
             copy_k(out=kT[:, h, :, c * TPC * HT:(c + 1) * TPC * HT].rearrange("p u (w i) -> p u w i", i=2),
                    in_=keys.rearrange("p (w u i) -> p u w i", u=2, i=2))
 
         def regroup_v(h, g):
-            nc.scalar.copy(out=v_grp[:, h, g].rearrange("p (c i) t -> p c t i", i=4),
-                           in_=v_raw[:, h, g].rearrange("p t (c i) -> p c t i", i=4))
+            dst = v_grp[:, h, g].rearrange("p (c i) t -> p c t i", i=4)
+            src = v_raw[:, h, g].rearrange("p t (c i) -> p c t i", i=4)
+            if h == 0:
+                nc.scalar.copy(out=dst, in_=src)
+            else:
+                nc.vector.tensor_copy(out=dst, in_=src)
 
         def words(row):
             return row[:, 0:D].bitcast(FP8X4)
@@ -381,11 +385,11 @@ def tile_multiheadattn_kernel(tc, q, k, v, layer_idx, out):
                 quantise_v(0, 2 * s + 1)
                 if s == 1:
                     move_v(0)
-            if 3 * NCH <= s < 5 * NCH:
-                g = NCH - 1 - (s - 3 * NCH) // 2
+            if 2 * NCH <= s < 4 * NCH:
+                g = NCH - 1 - (s - 2 * NCH) // 2
                 if not odd:
                     regroup_v(1, g)
                 else:
                     quantise_v(1, g)
-                if s == 5 * NCH - 1:
+                if s == 4 * NCH - 1:
                     move_v(1)

@@ -121,17 +121,15 @@ def tile_multiheadattn_kernel(tc, q, k, v, layer_idx, out):
             tp = live["tp", h, c]
             queries = tp[:, 0:TPC, :].rearrange("p j s -> p (j s)")
             keys = tp[:, TPC:2 * TPC, :].rearrange("p j s -> p (j s)")
-            i = chunks.index((h, c))
-            copy_q = nc.scalar.copy if i > 0 else nc.vector.tensor_copy
-            copy_k = nc.scalar.copy if i == 1 else nc.vector.tensor_copy
-            copy_q(out=qT[:, h, c * W:(c + 1) * W], in_=queries)
-            copy_k(out=kT[:, h, :, c * TPC * HT:(c + 1) * TPC * HT].rearrange("p u (w i) -> p u w i", i=2),
-                   in_=keys.rearrange("p (w u i) -> p u w i", u=2, i=2))
+            copy = nc.vector.tensor_copy if (h, c) == (0, 0) else nc.scalar.copy
+            copy(out=qT[:, h, c * W:(c + 1) * W], in_=queries)
+            copy(out=kT[:, h, :, c * TPC * HT:(c + 1) * TPC * HT].rearrange("p u (w i) -> p u w i", i=2),
+                 in_=keys.rearrange("p (w u i) -> p u w i", u=2, i=2))
 
         def regroup_v(h, g):
             dst = v_grp[:, h, g].rearrange("p (c i) t -> p c t i", i=4)
             src = v_raw[:, h, g].rearrange("p t (c i) -> p c t i", i=4)
-            if h == 0:
+            if h == 0 and g > 0:
                 nc.scalar.copy(out=dst, in_=src)
             else:
                 nc.vector.tensor_copy(out=dst, in_=src)
@@ -158,7 +156,7 @@ def tile_multiheadattn_kernel(tc, q, k, v, layer_idx, out):
         def back_scores(i, r0):
             h, c = chunks[i]
             if r0 == 0:
-                sb = ps_b.tile([P, TPC, P], F32)
+                sb = ps_b.tile([P, TPC, P], F32, tag="sb")
                 live["sb", i] = sb
             sb = live["sb", i]
             for r in range(r0, r0 + 2):
@@ -231,10 +229,14 @@ def tile_multiheadattn_kernel(tc, q, k, v, layer_idx, out):
             for u in range(2):
                 nc.tensor.transpose(out_[:, u, :], pairs[:, u * P:(u + 1) * P], ident_w[:])
 
+        size = {x: 2 for x in range(0, NQ - 2, 2)}
+        size[NQ - 2] = 1
+        size[NQ - 1] = 1
+
         def transpose_e(x):
-            et = ps_t.tile([P, 2, 2, P], F32, tag="tp")
+            et = ps_t.tile([P, size[x], 2, P], F32, tag="tp")
             live["et", x] = et
-            for j in range(2):
+            for j in range(size[x]):
                 transpose_words(et[:, j], live["e", x + j])
 
         def transpose_back(i):
@@ -243,10 +245,11 @@ def tile_multiheadattn_kernel(tc, q, k, v, layer_idx, out):
             transpose_words(et, live["eb", i])
 
         def copy_e(x):
-            ge = gpool.tile([P, 2, P, TPC], BF16, align_bytes=64)
+            ge = gpool.tile([P, size[x], P, TPC], BF16, align_bytes=64)
             live["ge", x] = ge
-            pairs = ge[:].rearrange("p j q t -> p (j q t)").bitcast(F32).rearrange("p (j q u) -> p j q u", j=2, u=2)
-            nc.scalar.copy(out=pairs, in_=live["et", x][:].rearrange("p j u q -> p j q u"))
+            pairs = ge[:].rearrange("p j q t -> p (j q t)").bitcast(F32)
+            nc.scalar.copy(out=pairs.rearrange("p (j q u) -> p j q u", j=size[x], u=2),
+                           in_=live["et", x][:].rearrange("p j u q -> p j q u"))
 
         def copy_back(i):
             geb = gpool.tile([P, P, TPC], BF16, align_bytes=64)
@@ -255,8 +258,8 @@ def tile_multiheadattn_kernel(tc, q, k, v, layer_idx, out):
             nc.scalar.copy(out=pairs, in_=live["etb", i][:].rearrange("p u q -> p q u"))
 
         def quantise_e(x):
-            cod = cpool.tile([P, 2 * P], U32, align_bytes=64)
-            scl = cpool.tile([P, 2 * P], U8, align_bytes=64)
+            cod = cpool.tile([P, size[x] * P], U32, align_bytes=64)
+            scl = cpool.tile([P, size[x] * P], U8, align_bytes=64)
             live["cod", x] = cod
             live["scl", x] = scl
             nc.vector.quantize_mx(out=cod[:].bitcast(FP8X4), scales=scl[:],
@@ -271,52 +274,61 @@ def tile_multiheadattn_kernel(tc, q, k, v, layer_idx, out):
                                   in_=live["geb", i][:].rearrange("p q t -> p (q t)"))
 
         def e_times_v(x):
-            acc = ps_o.tile([P, 2, D], F32, tag="acc")
+            if x in (NQ - 6, NQ - 2):
+                acc = ps_b.tile([P, size[x], D], F32, tag="sb")
+            else:
+                acc = ps_o.tile([P, size[x], D], F32, tag="acc")
             live["acc", x] = acc
-            for j in range(2):
+            for j in range(size[x]):
                 h, n = tiles[x + j]
                 c, r = n // TPC, n % TPC
                 row = v_qnt[:, h, c] if c == 0 or r == TPC - 1 else v_win[:, h, r, c - 1]
-                nc.tensor.matmul_mx(out=acc[:, n % 2, :], lhsT=live["cod", x][:, j * P:(j + 1) * P].bitcast(FP8X4),
+                nc.tensor.matmul_mx(out=acc[:, n % size[x], :], lhsT=live["cod", x][:, j * P:(j + 1) * P].bitcast(FP8X4),
                                     lhsT_scale=live["scl", x][:, j * P:(j + 1) * P],
                                     rhs=words(row), rhs_scale=scales(row), start=True, stop=c == 0)
                 if c > 0:
                     i = x // TPC
-                    nc.tensor.matmul_mx(out=acc[:, n % 2, :], lhsT=live["codb", i][:].bitcast(FP8X4),
+                    nc.tensor.matmul_mx(out=acc[:, n % size[x], :], lhsT=live["codb", i][:].bitcast(FP8X4),
                                         lhsT_scale=live["sclb", i][:], rhs=v_far[:, h, c - 1, r].bitcast(FP8X4),
                                         rhs_scale=scales(v_qnt[:, h, c - 1]), start=False, stop=True)
 
-        def first_of_two(x):
+        def lowest(x, count):
             h, n = tiles[x]
-            return h, n - n % 2
+            return h, min(n, tiles[x + count - 1][1])
 
-        def add_row_sums(x):
-            h, n = first_of_two(x)
-            rsm = small.tile([P, 2], F32)
+        def add_row_sums(x, count):
+            h, n = lowest(x, count)
+            rsm = small.tile([P, count], F32)
             live["rsm", x] = rsm
-            nc.gpsimd.tensor_tensor(out=rsm[:], in0=rs[:, h, n:n + 2, 0], in1=rs[:, h, n:n + 2, 1], op=ALU.add)
+            nc.gpsimd.tensor_tensor(out=rsm[:], in0=rs[:, h, n:n + count, 0], in1=rs[:, h, n:n + count, 1], op=ALU.add)
 
-        def invert_row_sums(x):
-            rcp = small.tile([P, 2], F32)
-            live["rcp", x] = rcp
+        def invert_row_sums(x, count):
+            rcp = small.tile([P, count], F32)
             nc.vector.reciprocal(rcp[:], live["rsm", x][:])
+            for y in range(x, x + count):
+                live["rcp", y] = rcp[:, tiles[y][1] - lowest(x, count)[1]:]
 
         def scale_and_store(x):
-            h, n = first_of_two(x)
-            osb = opool.tile([P, 2, D], F32)
+            h, n = lowest(x, size[x])
+            osb = opool.tile([P, size[x], D], F32)
+            rcp = live["rcp", x + size[x] - 1 if tiles[x][1] > n else x][:, 0:size[x]]
             nc.vector.tensor_tensor(out=osb[:], in0=live["acc", x][:],
-                                    in1=live["rcp", x][:].unsqueeze(2).to_broadcast([P, 2, D]), op=ALU.mult)
-            nc.sync.dma_start(out=ov[h][:, n:n + 2, :], in_=osb[:])
+                                    in1=rcp.unsqueeze(2).to_broadcast([P, size[x], D]), op=ALU.mult)
+            nc.sync.dma_start(out=ov[h][:, n:n + size[x], :], in_=osb[:])
 
         def has_back(i):
             return 0 <= i < NC and chunks[i][1] > 0
 
+        te_at = {x + size[x]: x for x in size}
         mx_at = {}
-        for x in range(0, NQ, 2):
-            step = x + 5 if not has_back(x // TPC) else x // TPC * TPC + 7 + x % TPC
-            while step in mx_at:
-                step += 1
-            mx_at[step] = x
+        for x in size:
+            i = x // TPC
+            last = x + size[x] + 1
+            if has_back(i):
+                last = max(last, TPC * i + TPC + 1)
+            gap = 1 if i >= NC - 2 else 2
+            mx_at[max([last + gap] + [s + gap for s in mx_at])] = x
+
         qk_at = {}
         step = TPC * NC
         for i in range(NC - 1, 0, -1):
@@ -338,8 +350,8 @@ def tile_multiheadattn_kernel(tc, q, k, v, layer_idx, out):
             regroup_v(0, g)
         for s in range(-2, max(mx_at) + 2):
             odd = s % 2 == 1
-            if 2 <= s <= NQ and not odd:
-                transpose_e(s - 2)
+            if s in te_at:
+                transpose_e(te_at[s])
             if s >= TPC and s % TPC == 0 and has_back(s // TPC - 1):
                 transpose_back(s // TPC - 1)
             if s in mx_at:
@@ -362,22 +374,26 @@ def tile_multiheadattn_kernel(tc, q, k, v, layer_idx, out):
                 copy_qk(*chunks[qk_at[s - 1]])
             if s - 1 in mx_at:
                 scale_and_store(mx_at[s - 1])
-            if 3 <= s <= NQ + 1 and odd:
-                quantise_e(s - 3)
+            if s - 1 in te_at:
+                quantise_e(te_at[s - 1])
             if s >= TPC + 1 and s % TPC == 1 and has_back(s // TPC - 1):
                 quantise_back(s // TPC - 1)
             if 0 <= s + 1 < NQ:
                 bias(s + 1)
-            if s + 1 in mx_at:
-                invert_row_sums(mx_at[s + 1])
-            if s + 2 in mx_at:
-                add_row_sums(mx_at[s + 2])
+            if s % TPC == 1 and 0 < s // TPC < NC:
+                invert_row_sums(s - TPC - 1, TPC)
+            if s + 1 in mx_at and mx_at[s + 1] >= NQ - TPC:
+                invert_row_sums(mx_at[s + 1], size[mx_at[s + 1]])
+            if s % TPC == 0 and 0 < s // TPC < NC:
+                add_row_sums(s - TPC, TPC)
+            if s + 2 in mx_at and mx_at[s + 2] >= NQ - TPC:
+                add_row_sums(mx_at[s + 2], size[mx_at[s + 2]])
             if 0 <= s < NQ:
                 exponentials(s)
             if s == 0:
                 copy_qk(*chunks[1])
-            if 2 <= s <= NQ and not odd:
-                copy_e(s - 2)
+            if s in te_at:
+                copy_e(te_at[s])
             if s >= TPC and s % TPC == 0 and has_back(s // TPC - 1):
                 copy_back(s // TPC - 1)
             if 0 <= s < 2:
@@ -385,11 +401,9 @@ def tile_multiheadattn_kernel(tc, q, k, v, layer_idx, out):
                 quantise_v(0, 2 * s + 1)
                 if s == 1:
                     move_v(0)
-            if 2 * NCH <= s < 4 * NCH:
-                g = NCH - 1 - (s - 2 * NCH) // 2
-                if not odd:
-                    regroup_v(1, g)
-                else:
-                    quantise_v(1, g)
-                if s == 4 * NCH - 1:
+            if 0 < s < TPC * NCH and s % TPC == 2:
+                regroup_v(1, NCH - 1 - s // TPC)
+            if 0 < s < TPC * NCH and s % TPC == 3:
+                quantise_v(1, NCH - 1 - s // TPC)
+                if s // TPC == NCH - 1:
                     move_v(1)

@@ -32,10 +32,10 @@ FLOPS = 2 * 2 * H * D * (W * W + (NCH - 1) * W * 2 * W)
 def tile_multiheadattn_kernel(tc, q, k, v, layer_idx, out):
     assert layer_idx % 2 == 1, "only the local mask of the odd layers is built"
     nc = tc.nc
-    qv = q.rearrange("b h (n p) d -> (b h) p n d", p=P)
-    kv = k.rearrange("b h (n p) d -> (b h) p n d", p=P)
+    qv = q.rearrange("b h (m p j) d -> (b h) p m j d", p=P, j=2)
+    kv = k.rearrange("b h (m p j) d -> (b h) p m j d", p=P, j=2)
     vv = v.rearrange("b h (g p t) d -> (b h) p g t d", p=P, t=TPC)
-    ov = out.rearrange("b h (n p) d -> (b h) p n d", p=P)
+    ov = out.rearrange("b h (n w j) d -> (b h) j w n d", w=HT, j=2)
 
     tiles = [(0, n) for n in range(NT)] + [(1, n) for n in range(NT - 1, -1, -1)]
     chunks = [(0, c) for c in range(NCH)] + [(1, c) for c in range(NCH - 1, -1, -1)]
@@ -53,8 +53,8 @@ def tile_multiheadattn_kernel(tc, q, k, v, layer_idx, out):
         ps_o = ctx.enter_context(tc.psum_pool(name="ps_o", bufs=1))
         ctx.enter_context(tc.manual_schedule())
 
-        q_raw = keep.tile([P, H, NT, D], BF16)
-        k_raw = keep.tile([P, H, NT, D], BF16)
+        q_raw = keep.tile([P, H, NT // 2, 2, D], BF16)
+        k_raw = keep.tile([P, H, NT // 2, 2, D], BF16)
         v_raw = keep.tile([P, H, NCH, TPC, D], BF16)
         qT = keep.tile([P, H, S], BF16)
         kT = keep.tile([P, H, 2, S // 2], BF16)
@@ -63,6 +63,7 @@ def tile_multiheadattn_kernel(tc, q, k, v, layer_idx, out):
         v_win = keep.tile([P, H, TPC - 1, NCH - 1, ROW], U32, align_bytes=64)
         v_far = keep.tile([P, H, NCH - 1, TPC, D], U32, align_bytes=64)
         ident = keep.tile([P, P], BF16)
+        ident_q = keep.tile([P, P], BF16)
         ident_w = keep.tile([P, P], F32)
         mask_f = keep.tile([P, 2, P], F32)
         mask_b = keep.tile([P, 2, P], BF16)
@@ -75,7 +76,7 @@ def tile_multiheadattn_kernel(tc, q, k, v, layer_idx, out):
             e_first.append(e_r)
 
         def load(queue, raw, view, h, c):
-            queue.dma_start(out=raw[:, h, c * TPC:(c + 1) * TPC, :], in_=view[h][:, c * TPC:(c + 1) * TPC, :])
+            queue.dma_start(out=raw[:, h, 2 * c:2 * c + 2], in_=view[h][:, 2 * c:2 * c + 2])
 
         load(nc.sync, k_raw, kv, 0, 0)
         load(nc.scalar, q_raw, qv, 0, 0)
@@ -103,32 +104,36 @@ def tile_multiheadattn_kernel(tc, q, k, v, layer_idx, out):
         nc.gpsimd.memset(v_far[:], 0)
         nc.vector.memset(rs[:], 0.0)
         nc.vector.memset(v_qnt[:, :, :, D:ROW].bitcast(I32), 0)
+        nc.vector.tensor_copy(out=ident_q[:].rearrange("p (j w) -> p j w", j=2),
+                              in_=ident[:].rearrange("p (w j) -> p j w", j=2))
         for y in range(2):
-            nc.vector.tensor_copy(out=mask_b[:, y, :].rearrange("p (u w i) -> p u w i", u=2, i=2),
-                                  in_=mask_f[:, y, :].rearrange("p (w u i) -> p u w i", u=2, i=2))
+            nc.vector.tensor_copy(out=mask_b[:, y, :].rearrange("p (u c) -> p u c", u=2),
+                                  in_=mask_f[:, y, :].rearrange("p (c u) -> p u c", u=2))
 
         live = {}
 
         def transpose_qk(h, c):
-            tp = ps_t.tile([P, 2 * TPC, P], BF16, tag="tp")
+            tp = ps_t.tile([P, 2, TPC * P], BF16, tag="tp")
             live["tp", h, c] = tp
-            for j in range(TPC):
-                nc.tensor.transpose(tp[:, j, :], q_raw[:, h, c * TPC + j, :], ident[:])
-            for j in range(TPC):
-                nc.tensor.transpose(tp[:, TPC + j, :], k_raw[:, h, c * TPC + j, :], ident[:])
+            queries = tp[:, 0].rearrange("p (m n j w) -> p m j n w", m=2, n=2, j=2)
+            keys = tp[:, 1].rearrange("p (u m w) -> p m u w", u=2, m=2)
+            for m in range(2):
+                for j in range(2):
+                    nc.tensor.transpose(queries[:, m, j], q_raw[:, h, 2 * c + m, j, :],
+                                        ident[:].rearrange("p (n w) -> p n w", n=2))
+            for m in range(2):
+                for u in range(2):
+                    nc.tensor.transpose(keys[:, m, u], k_raw[:, h, 2 * c + m, u, :], ident[:])
 
         def copy_qk(h, c):
             tp = live["tp", h, c]
-            queries = tp[:, 0:TPC, :].rearrange("p j s -> p (j s)")
-            keys = tp[:, TPC:2 * TPC, :].rearrange("p j s -> p (j s)")
             copy = nc.vector.tensor_copy if (h, c) == (0, 0) else nc.scalar.copy
-            copy(out=qT[:, h, c * W:(c + 1) * W], in_=queries)
-            copy(out=kT[:, h, :, c * TPC * HT:(c + 1) * TPC * HT].rearrange("p u (w i) -> p u w i", i=2),
-                 in_=keys.rearrange("p (w u i) -> p u w i", u=2, i=2))
+            copy(out=qT[:, h, c * W:(c + 1) * W], in_=tp[:, 0])
+            copy(out=kT[:, h, :, c * TPC * HT:(c + 1) * TPC * HT], in_=tp[:, 1].rearrange("p (u s) -> p u s", u=2))
 
         def regroup_v(h, g):
-            dst = v_grp[:, h, g].rearrange("p (c i) t -> p c t i", i=4)
-            src = v_raw[:, h, g].rearrange("p t (c i) -> p c t i", i=4)
+            dst = v_grp[:, h, g].rearrange("p d (u i) -> p d u i", u=2)
+            src = v_raw[:, h, g].rearrange("p (i u) d -> p d u i", u=2)
             if h == 0 and g > 0:
                 nc.scalar.copy(out=dst, in_=src)
             else:
@@ -161,7 +166,7 @@ def tile_multiheadattn_kernel(tc, q, k, v, layer_idx, out):
             sb = live["sb", i]
             for r in range(r0, r0 + 2):
                 n = c * TPC + r
-                nc.tensor.matmul(sb[:, r, :], lhsT=ident[:], rhs=mask_b[:, 1, :], start=True, stop=False)
+                nc.tensor.matmul(sb[:, r, :], lhsT=ident_q[:], rhs=mask_b[:, 1, :], start=True, stop=False)
                 nc.tensor.matmul(sb[:, r, :].rearrange("p (u s) -> p u s", u=2), lhsT=qT[:, h, n * P:(n + 1) * P],
                                  rhs=kT[:, h, :, (n - TPC) * HT:(n - TPC + 1) * HT], start=False, stop=True)
 
@@ -181,7 +186,7 @@ def tile_multiheadattn_kernel(tc, q, k, v, layer_idx, out):
                                  start=True, stop=True)
             nc.tensor.matmul(sa[:, :, 0:(r + 1) * HT], lhsT=rows, rhs=kT[:, h, :, c * TPC * HT:(n + 1) * HT],
                              start=True, stop=False)
-            nc.tensor.matmul(sa[:, :, r * HT:(r + 1) * HT], lhsT=ident[:],
+            nc.tensor.matmul(sa[:, :, r * HT:(r + 1) * HT], lhsT=ident_q[:],
                              rhs=mask_b[:, 0, :].rearrange("p (u s) -> p u s", u=2), start=False, stop=True)
 
         def columns(n):
@@ -314,7 +319,8 @@ def tile_multiheadattn_kernel(tc, q, k, v, layer_idx, out):
             rcp = live["rcp", x + size[x] - 1 if tiles[x][1] > n else x][:, 0:size[x]]
             nc.vector.tensor_tensor(out=osb[:], in0=live["acc", x][:],
                                     in1=rcp.unsqueeze(2).to_broadcast([P, size[x], D]), op=ALU.mult)
-            nc.sync.dma_start(out=ov[h][:, n:n + size[x], :], in_=osb[:])
+            for j in range(2):
+                nc.sync.dma_start(out=ov[h][j][:, n:n + size[x], :], in_=osb[HT * j:HT * (j + 1)])
 
         def has_back(i):
             return 0 <= i < NC and chunks[i][1] > 0
@@ -401,9 +407,11 @@ def tile_multiheadattn_kernel(tc, q, k, v, layer_idx, out):
                 quantise_v(0, 2 * s + 1)
                 if s == 1:
                     move_v(0)
-            if 0 < s < TPC * NCH and s % TPC == 2:
-                regroup_v(1, NCH - 1 - s // TPC)
-            if 0 < s < TPC * NCH and s % TPC == 3:
-                quantise_v(1, NCH - 1 - s // TPC)
-                if s // TPC == NCH - 1:
+            if 2 * NCH <= s < 4 * NCH:
+                g = NCH - 1 - (s - 2 * NCH) // 2
+                if not odd:
+                    regroup_v(1, g)
+                else:
+                    quantise_v(1, g)
+                if s == 4 * NCH - 1:
                     move_v(1)

@@ -32,10 +32,10 @@ FLOPS = 2 * 2 * H * D * (W * W + (NCH - 1) * W * 2 * W)
 def tile_multiheadattn_kernel(tc, q, k, v, layer_idx, out):
     assert layer_idx % 2 == 1, "only the local mask of the odd layers is built"
     nc = tc.nc
-    qv = q.rearrange("b h (m p j) d -> (b h) p m j d", p=P, j=2)
-    kv = k.rearrange("b h (m p j) d -> (b h) p m j d", p=P, j=2)
+    qv = q.rearrange("b h (n p) d -> (b h) p n d", p=P)
+    kv = k.rearrange("b h (m p u) d -> (b h) p m u d", p=P, u=2)
     vv = v.rearrange("b h (g p t) d -> (b h) p g t d", p=P, t=TPC)
-    ov = out.rearrange("b h (n w j) d -> (b h) j w n d", w=HT, j=2)
+    ov = out.rearrange("b h (n p) d -> (b h) p n d", p=P)
 
     tiles = [(0, n) for n in range(NT)] + [(1, n) for n in range(NT - 1, -1, -1)]
     chunks = [(0, c) for c in range(NCH)] + [(1, c) for c in range(NCH - 1, -1, -1)]
@@ -53,17 +53,15 @@ def tile_multiheadattn_kernel(tc, q, k, v, layer_idx, out):
         ps_o = ctx.enter_context(tc.psum_pool(name="ps_o", bufs=1))
         ctx.enter_context(tc.manual_schedule())
 
-        q_raw = keep.tile([P, H, NT // 2, 2, D], BF16)
+        q_raw = keep.tile([P, H, NT, D], BF16)
         k_raw = keep.tile([P, H, NT // 2, 2, D], BF16)
         v_raw = keep.tile([P, H, NCH, TPC, D], BF16)
-        qT = keep.tile([P, H, S], BF16)
-        kT = keep.tile([P, H, 2, S // 2], BF16)
+        qkT = keep.tile([P, H, NCH, 2, W], BF16)
         v_grp = keep.tile([P, H, NCH, D, TPC], BF16, align_bytes=64)
         v_qnt = keep.tile([P, H, NCH, ROW], U32, align_bytes=64)
         v_win = keep.tile([P, H, TPC - 1, NCH - 1, ROW], U32, align_bytes=64)
         v_far = keep.tile([P, H, NCH - 1, TPC, D], U32, align_bytes=64)
         ident = keep.tile([P, P], BF16)
-        ident_q = keep.tile([P, P], BF16)
         ident_w = keep.tile([P, P], F32)
         mask_f = keep.tile([P, 2, P], F32)
         mask_b = keep.tile([P, 2, P], BF16)
@@ -75,17 +73,20 @@ def tile_multiheadattn_kernel(tc, q, k, v, layer_idx, out):
             e_r = keep.tile([P, 2, TPC * HT], BF16, name="e%d" % r)
             e_first.append(e_r)
 
-        def load(queue, raw, view, h, c):
-            queue.dma_start(out=raw[:, h, 2 * c:2 * c + 2], in_=view[h][:, 2 * c:2 * c + 2])
+        def load_q(queue, h, c):
+            queue.dma_start(out=q_raw[:, h, c * TPC:(c + 1) * TPC], in_=qv[h][:, c * TPC:(c + 1) * TPC])
 
-        load(nc.sync, k_raw, kv, 0, 0)
-        load(nc.scalar, q_raw, qv, 0, 0)
+        def load_k(h, c):
+            nc.sync.dma_start(out=k_raw[:, h, 2 * c:2 * c + 2], in_=kv[h][:, 2 * c:2 * c + 2])
+
+        load_k(0, 0)
+        load_q(nc.scalar, 0, 0)
         for g in range(NCH):
             nc.sync.dma_start(out=v_raw[:, 0, g], in_=vv[0][:, g])
         for x, (h, c) in enumerate(chunks):
             if x > 0:
-                load(nc.sync, k_raw, kv, h, c)
-                load(nc.sync, q_raw, qv, h, c)
+                load_k(h, c)
+                load_q(nc.sync, h, c)
             if x == NCH:
                 nc.sync.dma_start(out=v_raw[:, 1], in_=vv[1])
 
@@ -104,8 +105,6 @@ def tile_multiheadattn_kernel(tc, q, k, v, layer_idx, out):
         nc.gpsimd.memset(v_far[:], 0)
         nc.vector.memset(rs[:], 0.0)
         nc.vector.memset(v_qnt[:, :, :, D:ROW].bitcast(I32), 0)
-        nc.vector.tensor_copy(out=ident_q[:].rearrange("p (j w) -> p j w", j=2),
-                              in_=ident[:].rearrange("p (w j) -> p j w", j=2))
         for y in range(2):
             nc.vector.tensor_copy(out=mask_b[:, y, :].rearrange("p (u c) -> p u c", u=2),
                                   in_=mask_f[:, y, :].rearrange("p (c u) -> p u c", u=2))
@@ -113,23 +112,24 @@ def tile_multiheadattn_kernel(tc, q, k, v, layer_idx, out):
         live = {}
 
         def transpose_qk(h, c):
-            tp = ps_t.tile([P, 2, TPC * P], BF16, tag="tp")
+            tp = ps_t.tile([P, 2, W], BF16, tag="tp")
             live["tp", h, c] = tp
-            queries = tp[:, 0].rearrange("p (m n j w) -> p m j n w", m=2, n=2, j=2)
             keys = tp[:, 1].rearrange("p (u m w) -> p m u w", u=2, m=2)
-            for m in range(2):
-                for j in range(2):
-                    nc.tensor.transpose(queries[:, m, j], q_raw[:, h, 2 * c + m, j, :],
-                                        ident[:].rearrange("p (n w) -> p n w", n=2))
+            for r in range(TPC):
+                nc.tensor.transpose(tp[:, 0, r * P:(r + 1) * P], q_raw[:, h, c * TPC + r, :], ident[:])
             for m in range(2):
                 for u in range(2):
                     nc.tensor.transpose(keys[:, m, u], k_raw[:, h, 2 * c + m, u, :], ident[:])
 
         def copy_qk(h, c):
-            tp = live["tp", h, c]
             copy = nc.vector.tensor_copy if (h, c) == (0, 0) else nc.scalar.copy
-            copy(out=qT[:, h, c * W:(c + 1) * W], in_=tp[:, 0])
-            copy(out=kT[:, h, :, c * TPC * HT:(c + 1) * TPC * HT], in_=tp[:, 1].rearrange("p (u s) -> p u s", u=2))
+            copy(out=qkT[:, h, c], in_=live["tp", h, c][:])
+
+        def queries_of(h, n):
+            return qkT[:, h, n // TPC, 0, n % TPC * P:(n % TPC + 1) * P]
+
+        def keys_of(h, c, r0, r1):
+            return qkT[:, h, c, 1].rearrange("p (u x) -> p u x", u=2)[:, :, r0 * HT:r1 * HT]
 
         def regroup_v(h, g):
             dst = v_grp[:, h, g].rearrange("p d (u i) -> p d u i", u=2)
@@ -166,9 +166,9 @@ def tile_multiheadattn_kernel(tc, q, k, v, layer_idx, out):
             sb = live["sb", i]
             for r in range(r0, r0 + 2):
                 n = c * TPC + r
-                nc.tensor.matmul(sb[:, r, :], lhsT=ident_q[:], rhs=mask_b[:, 1, :], start=True, stop=False)
-                nc.tensor.matmul(sb[:, r, :].rearrange("p (u s) -> p u s", u=2), lhsT=qT[:, h, n * P:(n + 1) * P],
-                                 rhs=kT[:, h, :, (n - TPC) * HT:(n - TPC + 1) * HT], start=False, stop=True)
+                nc.tensor.matmul(sb[:, r, :], lhsT=ident[:], rhs=mask_b[:, 1, :], start=True, stop=False)
+                nc.tensor.matmul(sb[:, r, :].rearrange("p (u s) -> p u s", u=2), lhsT=queries_of(h, n),
+                                 rhs=keys_of(h, c - 1, r, r + 1), start=False, stop=True)
 
         def back_max(i):
             rb = small.tile([P, TPC], F32)
@@ -180,13 +180,13 @@ def tile_multiheadattn_kernel(tc, q, k, v, layer_idx, out):
             c, r = n // TPC, n % TPC
             sa = ps_a.tile([P, 2, TPC * HT], F32)
             live["sa", x] = sa
-            rows = qT[:, h, n * P:(n + 1) * P]
+            rows = queries_of(h, n)
             if c > 0 and r < TPC - 1:
-                nc.tensor.matmul(sa[:, :, (r + 1) * HT:], lhsT=rows, rhs=kT[:, h, :, (n - TPC + 1) * HT:c * TPC * HT],
+                nc.tensor.matmul(sa[:, :, (r + 1) * HT:], lhsT=rows, rhs=keys_of(h, c - 1, r + 1, TPC),
                                  start=True, stop=True)
-            nc.tensor.matmul(sa[:, :, 0:(r + 1) * HT], lhsT=rows, rhs=kT[:, h, :, c * TPC * HT:(n + 1) * HT],
+            nc.tensor.matmul(sa[:, :, 0:(r + 1) * HT], lhsT=rows, rhs=keys_of(h, c, 0, r + 1),
                              start=True, stop=False)
-            nc.tensor.matmul(sa[:, :, r * HT:(r + 1) * HT], lhsT=ident_q[:],
+            nc.tensor.matmul(sa[:, :, r * HT:(r + 1) * HT], lhsT=ident[:],
                              rhs=mask_b[:, 0, :].rearrange("p (u s) -> p u s", u=2), start=False, stop=True)
 
         def columns(n):
@@ -260,7 +260,7 @@ def tile_multiheadattn_kernel(tc, q, k, v, layer_idx, out):
             geb = gpool.tile([P, P, TPC], BF16, align_bytes=64)
             live["geb", i] = geb
             pairs = geb[:].rearrange("p q t -> p (q t)").bitcast(F32).rearrange("p (q u) -> p q u", u=2)
-            nc.scalar.copy(out=pairs, in_=live["etb", i][:].rearrange("p u q -> p q u"))
+            nc.vector.tensor_copy(out=pairs, in_=live["etb", i][:].rearrange("p u q -> p q u"))
 
         def quantise_e(x):
             cod = cpool.tile([P, size[x] * P], U32, align_bytes=64)
@@ -319,8 +319,7 @@ def tile_multiheadattn_kernel(tc, q, k, v, layer_idx, out):
             rcp = live["rcp", x + size[x] - 1 if tiles[x][1] > n else x][:, 0:size[x]]
             nc.vector.tensor_tensor(out=osb[:], in0=live["acc", x][:],
                                     in1=rcp.unsqueeze(2).to_broadcast([P, size[x], D]), op=ALU.mult)
-            for j in range(2):
-                nc.sync.dma_start(out=ov[h][j][:, n:n + size[x], :], in_=osb[HT * j:HT * (j + 1)])
+            nc.sync.dma_start(out=ov[h][:, n:n + size[x], :], in_=osb[:])
 
         def has_back(i):
             return 0 <= i < NC and chunks[i][1] > 0
@@ -407,11 +406,11 @@ def tile_multiheadattn_kernel(tc, q, k, v, layer_idx, out):
                 quantise_v(0, 2 * s + 1)
                 if s == 1:
                     move_v(0)
-            if 2 * NCH <= s < 4 * NCH:
-                g = NCH - 1 - (s - 2 * NCH) // 2
-                if not odd:
-                    regroup_v(1, g)
-                else:
-                    quantise_v(1, g)
-                if s == 4 * NCH - 1:
+            g = NCH + 1 - s // 3
+            if s % 3 == 0 and 0 <= g < NCH:
+                regroup_v(1, g)
+            g = NCH + 1 - (s - 1) // 3
+            if s % 3 == 1 and 0 <= g < NCH:
+                quantise_v(1, g)
+                if g == 0:
                     move_v(1)

@@ -91,7 +91,7 @@ def tile_multiheadattn_kernel(tc, q, k, v, layer_idx, out):
                 nc.sync.dma_start(out=v_raw[:, 1], in_=vv[1])
 
         make_identity(nc, ident[:])
-        nc.vector.memset(zeros[:], 0.0)
+        nc.vector.memset(zeros[:].bitcast(I32), 0)
         nc.vector.memset(warm[:, 0:1], 0.0)
         nc.scalar.activation(out=warm[:, 1:2], in_=warm[:, 0:1], func=ACT.Exp)
         nc.gpsimd.memset(mask_f[:], 0.0)
@@ -101,8 +101,8 @@ def tile_multiheadattn_kernel(tc, q, k, v, layer_idx, out):
                                 base=-1, pattern=[[1, P]], channel_multiplier=-1)
         make_identity(nc, ident_w[:])
         for r in range(TPC - 1):
-            nc.gpsimd.memset(e_first[r][:, :, HT * (r + 1):], 0.0)
-        nc.gpsimd.memset(v_far[:], 0)
+            nc.vector.memset(e_first[r][:, :, HT * (r + 1):], 0.0)
+        nc.vector.memset(v_far[:], 0)
         nc.vector.memset(rs[:], 0.0)
         nc.vector.memset(v_qnt[:, :, :, D:ROW].bitcast(I32), 0)
         for y in range(2):

from contextlib import ExitStack
import math

import concourse.mybir as mybir
from concourse.masks import make_identity

F32 = mybir.dt.float32
BF16 = mybir.dt.bfloat16
I32 = mybir.dt.int32
U32 = mybir.dt.uint32
U8 = mybir.dt.uint8
FP8X4 = mybir.dt.float8_e4m3fn_x4
ALU = mybir.AluOpType
ACT = mybir.ActivationFunctionType
AX = mybir.AxisListType

H, S, D, W = 2, 2048, 128, 512
P = 128
HT = P // 2
NT = S // P
TPC = W // P
QP = P // TPC
NCH = S // W
NQ = H * NT
NC = H * NCH
SCALE = 1.0 / math.sqrt(D)
MASKED = -17179869184.0
ROW = D + D // 4
FLOPS = 2 * 2 * H * D * (W * W + (NCH - 1) * W * 2 * W)


def tile_multiheadattn_kernel(tc, q, k, v, layer_idx, out):
    assert layer_idx % 2 == 1, "only the local mask of the odd layers is built"
    nc = tc.nc
    qv = q.rearrange("b h (n p) d -> (b h) p n d", p=P)
    kv = k.rearrange("b h (m p u) d -> (b h) p m u d", p=P, u=2)
    vv = v.rearrange("b h (g p t) d -> (b h) p g t d", p=P, t=TPC)
    ov = out.rearrange("b h (n p) d -> (b h) p n d", p=P)

    tiles = [(0, n) for n in range(NT)] + [(1, n) for n in range(NT - 1, -1, -1)]
    chunks = [(0, c) for c in range(NCH)] + [(1, c) for c in range(NCH - 1, -1, -1)]

    with ExitStack() as ctx:
        keep = ctx.enter_context(tc.tile_pool(name="keep", bufs=1))
        small = ctx.enter_context(tc.tile_pool(name="small", bufs=12))
        epool = ctx.enter_context(tc.tile_pool(name="epool", bufs=4))
        gpool = ctx.enter_context(tc.tile_pool(name="gpool", bufs=3))
        cpool = ctx.enter_context(tc.tile_pool(name="cpool", bufs=5))
        opool = ctx.enter_context(tc.tile_pool(name="opool", bufs=6))
        ps_a = ctx.enter_context(tc.psum_pool(name="ps_a", bufs=3))
        ps_b = ctx.enter_context(tc.psum_pool(name="ps_b", bufs=2))
        ps_t = ctx.enter_context(tc.psum_pool(name="ps_t", bufs=2))
        ps_o = ctx.enter_context(tc.psum_pool(name="ps_o", bufs=1))
        ctx.enter_context(tc.manual_schedule())

        q_raw = keep.tile([P, H, NT, D], BF16)
        k_raw = keep.tile([P, H, NT // 2, 2, D], BF16)
        v_raw = keep.tile([P, H, NCH, TPC, D], BF16)
        qkT = keep.tile([P, H, NCH, 2, W], BF16)
        v_grp = keep.tile([P, H, NCH, D, TPC], BF16, align_bytes=64)
        v_qnt = keep.tile([P, H, NCH, ROW], U32, align_bytes=64)
        v_win = keep.tile([P, H, TPC - 1, NCH - 1, ROW], U32, align_bytes=64)
        v_far = keep.tile([P, H, NCH - 1, TPC, D], U32, align_bytes=64)
        ident = keep.tile([P, P], BF16)
        ident_w = keep.tile([P, P], F32)
        mask_f = keep.tile([P, 2, P], F32)
        mask_b = keep.tile([P, 2, P], BF16)
        warm = keep.tile([P, 2], F32)
        zeros = keep.tile([P, W], BF16)
        rs = keep.tile([P, H, NT, 2], F32)
        e_first = []
        for r in range(TPC):
            e_r = keep.tile([P, 2, TPC * HT], BF16, name="e%d" % r)
            e_first.append(e_r)

        def load_q(queue, h, c):
            queue.dma_start(out=q_raw[:, h, c * TPC:(c + 1) * TPC], in_=qv[h][:, c * TPC:(c + 1) * TPC])

        def load_k(h, c):
            nc.sync.dma_start(out=k_raw[:, h, 2 * c:2 * c + 2], in_=kv[h][:, 2 * c:2 * c + 2])

        load_k(0, 0)
        load_q(nc.scalar, 0, 0)
        for g in range(NCH):
            nc.sync.dma_start(out=v_raw[:, 0, g], in_=vv[0][:, g])
        for x, (h, c) in enumerate(chunks):
            if x > 0:
                load_k(h, c)
                load_q(nc.sync, h, c)
            if x == NCH:
                nc.sync.dma_start(out=v_raw[:, 1], in_=vv[1])

        make_identity(nc, ident[:])
        nc.vector.memset(zeros[:].bitcast(I32), 0)
        nc.vector.memset(warm[:, 0:1], 0.0)
        nc.scalar.activation(out=warm[:, 1:2], in_=warm[:, 0:1], func=ACT.Exp)
        nc.gpsimd.memset(mask_f[:], 0.0)
        nc.gpsimd.affine_select(out=mask_f[:, 0, :], in_=mask_f[:, 0, :], compare_op=ALU.is_ge, fill=MASKED,
                                base=0, pattern=[[-1, P]], channel_multiplier=1)
        nc.gpsimd.affine_select(out=mask_f[:, 1, :], in_=mask_f[:, 1, :], compare_op=ALU.is_ge, fill=MASKED,
                                base=-1, pattern=[[1, P]], channel_multiplier=-1)
        make_identity(nc, ident_w[:])
        for r in range(TPC - 1):
            nc.vector.memset(e_first[r][:, :, HT * (r + 1):], 0.0)
        nc.vector.memset(v_far[:], 0)
        nc.vector.memset(rs[:], 0.0)
        nc.vector.memset(v_qnt[:, :, :, D:ROW].bitcast(I32), 0)
        for y in range(2):
            nc.vector.tensor_copy(out=mask_b[:, y, :].rearrange("p (u c) -> p u c", u=2),
                                  in_=mask_f[:, y, :].rearrange("p (c u) -> p u c", u=2))

        live = {}

        def transpose_qk(h, c):
            tp = ps_t.tile([P, 2, W], BF16, tag="tp")
            live["tp", h, c] = tp
            keys = tp[:, 1].rearrange("p (u m w) -> p m u w", u=2, m=2)
            for r in range(TPC):
                nc.tensor.transpose(tp[:, 0, r * P:(r + 1) * P], q_raw[:, h, c * TPC + r, :], ident[:])
            for m in range(2):
                for u in range(2):
                    nc.tensor.transpose(keys[:, m, u], k_raw[:, h, 2 * c + m, u, :], ident[:])

        def copy_qk(h, c):
            copy = nc.vector.tensor_copy if (h, c) == (0, 0) else nc.scalar.copy
            copy(out=qkT[:, h, c], in_=live["tp", h, c][:])

        def queries_of(h, n):
            return qkT[:, h, n // TPC, 0, n % TPC * P:(n % TPC + 1) * P]

        def keys_of(h, c, r0, r1):
            return qkT[:, h, c, 1].rearrange("p (u x) -> p u x", u=2)[:, :, r0 * HT:r1 * HT]

        def regroup_v(h, g):
            dst = v_grp[:, h, g].rearrange("p d (u i) -> p d u i", u=2)
            src = v_raw[:, h, g].rearrange("p (i u) d -> p d u i", u=2)
            if h == 0 and g > 0:
                nc.scalar.copy(out=dst, in_=src)
            else:
                nc.vector.tensor_copy(out=dst, in_=src)

        def words(row):
            return row[:, 0:D].bitcast(FP8X4)

        def scales(row):
            return row[:, D:ROW].bitcast(U8)

        def quantise_v(h, g):
            nc.vector.quantize_mx(out=words(v_qnt[:, h, g]), scales=scales(v_qnt[:, h, g]),
                                  in_=v_grp[:, h, g].rearrange("p d t -> p (d t)"))

        def move_v(h):
            for r in range(TPC - 1):
                own = QP * (r + 1)
                nc.sync.dma_start(out=v_win[0:own, h, r].bitcast(I32), in_=v_qnt[0:own, h, 1:NCH].bitcast(I32))
                nc.sync.dma_start(out=v_win[own:P, h, r].bitcast(I32), in_=v_qnt[own:P, h, 0:NCH - 1].bitcast(I32))
            for r in range(TPC):
                nc.sync.dma_start(out=v_far[QP * r:QP * (r + 1), h, :, r, :].bitcast(I32),
                                  in_=v_qnt[QP * r:QP * (r + 1), h, 0:NCH - 1, 0:D].bitcast(I32))

        def back_scores(i, r0):
            h, c = chunks[i]
            if r0 == 0:
                sb = ps_b.tile([P, TPC, P], F32, tag="sb")
                live["sb", i] = sb
            sb = live["sb", i]
            for r in range(r0, r0 + 2):
                n = c * TPC + r
                nc.tensor.matmul(sb[:, r, :], lhsT=ident[:], rhs=mask_b[:, 1, :], start=True, stop=False)
                nc.tensor.matmul(sb[:, r, :].rearrange("p (u s) -> p u s", u=2), lhsT=queries_of(h, n),
                                 rhs=keys_of(h, c - 1, r, r + 1), start=False, stop=True)

        def back_max(i):
            rb = small.tile([P, TPC], F32)
            live["rb", i] = rb
            nc.vector.tensor_reduce(out=rb[:], in_=live["sb", i][:], axis=AX.X, op=ALU.max)

        def near_scores(x):
            h, n = tiles[x]
            c, r = n // TPC, n % TPC
            sa = ps_a.tile([P, 2, TPC * HT], F32)
            live["sa", x] = sa
            rows = queries_of(h, n)
            if c > 0 and r < TPC - 1:
                nc.tensor.matmul(sa[:, :, (r + 1) * HT:], lhsT=rows, rhs=keys_of(h, c - 1, r + 1, TPC),
                                 start=True, stop=True)
            nc.tensor.matmul(sa[:, :, 0:(r + 1) * HT], lhsT=rows, rhs=keys_of(h, c, 0, r + 1),
                             start=True, stop=False)
            nc.tensor.matmul(sa[:, :, r * HT:(r + 1) * HT], lhsT=ident[:],
                             rhs=mask_b[:, 0, :].rearrange("p (u s) -> p u s", u=2), start=False, stop=True)

        def columns(n):
            return TPC * HT if n >= TPC else (n + 1) * HT

        def near_max(x):
            h, n = tiles[x]
            ra = small.tile([P, 1], F32)
            live["ra", x] = ra
            nc.vector.tensor_reduce(out=ra[:], in_=live["sa", x][:, :, 0:columns(n)], axis=AX.XY, op=ALU.max)

        def bias(x):
            h, n = tiles[x]
            nb = small.tile([P, 1], F32)
            live["nb", x] = nb
            if n < TPC:
                nc.vector.tensor_scalar(out=nb[:], in0=live["ra", x][:], scalar1=-SCALE, scalar2=None, op0=ALU.mult)
            else:
                rb = live["rb", x // TPC]
                nc.vector.tensor_scalar(out=nb[:], in0=live["ra", x][:], scalar1=rb[:, n % TPC:n % TPC + 1],
                                        scalar2=-SCALE, op0=ALU.max, op1=ALU.mult)

        def exponentials(x):
            h, n = tiles[x]
            r = n % TPC
            nb = live["nb", x]
            if n < TPC:
                e = e_first[n]
            else:
                e = epool.tile([P, 2, TPC * HT], BF16)
            live["e", x] = e
            nc.scalar.activation(out=e[:, :, 0:columns(n)], in_=live["sa", x][:, :, 0:columns(n)], func=ACT.Exp,
                                 bias=nb[:], scale=SCALE, accum_out=rs[:, h, n, 0:1])
            if n >= TPC:
                if x % TPC == 0:
                    eb = epool.tile([P, 2, TPC * HT], BF16)
                    live["eb", x // TPC] = eb
                eb = live["eb", x // TPC]
                nc.scalar.activation(out=eb[:, :, r * HT:(r + 1) * HT],
                                     in_=live["sb", x // TPC][:, r, :].rearrange("p (u s) -> p u s", u=2),
                                     func=ACT.Exp, bias=nb[:], scale=SCALE, accum_out=rs[:, h, n, 1:2])

        def transpose_words(out_, e):
            pairs = e[:].rearrange("p u s -> p (u s)").bitcast(F32)
            for u in range(2):
                nc.tensor.transpose(out_[:, u, :], pairs[:, u * P:(u + 1) * P], ident_w[:])

        size = {x: 2 for x in range(0, NQ - 2, 2)}
        size[NQ - 2] = 1
        size[NQ - 1] = 1

        def transpose_e(x):
            et = ps_t.tile([P, size[x], 2, P], F32, tag="tp")
            live["et", x] = et
            for j in range(size[x]):
                transpose_words(et[:, j], live["e", x + j])

        def transpose_back(i):
            et = ps_t.tile([P, 2, P], F32, tag="tp")
            live["etb", i] = et
            transpose_words(et, live["eb", i])

        def copy_e(x):
            ge = gpool.tile([P, size[x], P, TPC], BF16, align_bytes=64)
            live["ge", x] = ge
            pairs = ge[:].rearrange("p j q t -> p (j q t)").bitcast(F32)
            nc.scalar.copy(out=pairs.rearrange("p (j q u) -> p j q u", j=size[x], u=2),
                           in_=live["et", x][:].rearrange("p j u q -> p j q u"))

        def copy_back(i):
            geb = gpool.tile([P, P, TPC], BF16, align_bytes=64)
            live["geb", i] = geb
            pairs = geb[:].rearrange("p q t -> p (q t)").bitcast(F32).rearrange("p (q u) -> p q u", u=2)
            nc.vector.tensor_copy(out=pairs, in_=live["etb", i][:].rearrange("p u q -> p q u"))

        def quantise_e(x):
            cod = cpool.tile([P, size[x] * P], U32, align_bytes=64)
            scl = cpool.tile([P, size[x] * P], U8, align_bytes=64)
            live["cod", x] = cod
            live["scl", x] = scl
            nc.vector.quantize_mx(out=cod[:].bitcast(FP8X4), scales=scl[:],
                                  in_=live["ge", x][:].rearrange("p j q t -> p (j q t)"))

        def quantise_back(i):
            codb = cpool.tile([P, P], U32, align_bytes=64)
            sclb = cpool.tile([P, P], U8, align_bytes=64)
            live["codb", i] = codb
            live["sclb", i] = sclb
            nc.vector.quantize_mx(out=codb[:].bitcast(FP8X4), scales=sclb[:],
                                  in_=live["geb", i][:].rearrange("p q t -> p (q t)"))

        def e_times_v(x):
            if x in (NQ - 6, NQ - 2):
                acc = ps_b.tile([P, size[x], D], F32, tag="sb")
            else:
                acc = ps_o.tile([P, size[x], D], F32, tag="acc")
            live["acc", x] = acc
            for j in range(size[x]):
                h, n = tiles[x + j]
                c, r = n // TPC, n % TPC
                row = v_qnt[:, h, c] if c == 0 or r == TPC - 1 else v_win[:, h, r, c - 1]
                nc.tensor.matmul_mx(out=acc[:, n % size[x], :], lhsT=live["cod", x][:, j * P:(j + 1) * P].bitcast(FP8X4),
                                    lhsT_scale=live["scl", x][:, j * P:(j + 1) * P],
                                    rhs=words(row), rhs_scale=scales(row), start=True, stop=c == 0)
                if c > 0:
                    i = x // TPC
                    nc.tensor.matmul_mx(out=acc[:, n % size[x], :], lhsT=live["codb", i][:].bitcast(FP8X4),
                                        lhsT_scale=live["sclb", i][:], rhs=v_far[:, h, c - 1, r].bitcast(FP8X4),
                                        rhs_scale=scales(v_qnt[:, h, c - 1]), start=False, stop=True)

        def lowest(x, count):
            h, n = tiles[x]
            return h, min(n, tiles[x + count - 1][1])

        def add_row_sums(x, count):
            h, n = lowest(x, count)
            rsm = small.tile([P, count], F32)
            live["rsm", x] = rsm
            nc.gpsimd.tensor_tensor(out=rsm[:], in0=rs[:, h, n:n + count, 0], in1=rs[:, h, n:n + count, 1], op=ALU.add)

        def invert_row_sums(x, count):
            rcp = small.tile([P, count], F32)
            nc.vector.reciprocal(rcp[:], live["rsm", x][:])
            for y in range(x, x + count):
                live["rcp", y] = rcp[:, tiles[y][1] - lowest(x, count)[1]:]

        def scale_and_store(x):
            h, n = lowest(x, size[x])
            osb = opool.tile([P, size[x], D], F32)
            rcp = live["rcp", x + size[x] - 1 if tiles[x][1] > n else x][:, 0:size[x]]
            nc.vector.tensor_tensor(out=osb[:], in0=live["acc", x][:],
                                    in1=rcp.unsqueeze(2).to_broadcast([P, size[x], D]), op=ALU.mult)
            nc.sync.dma_start(out=ov[h][:, n:n + size[x], :], in_=osb[:])

        def has_back(i):
            return 0 <= i < NC and chunks[i][1] > 0

        te_at = {x + size[x]: x for x in size}
        mx_at = {}
        for x in size:
            i = x // TPC
            last = x + size[x] + 1
            if has_back(i):
                last = max(last, TPC * i + TPC + 1)
            gap = 1 if i >= NC - 2 else 2
            mx_at[max([last + gap] + [s + gap for s in mx_at])] = x

        qk_at = {}
        step = TPC * NC
        for i in range(NC - 1, 0, -1):
            needed = TPC * i - TPC if i <= NCH else TPC * i - 2 * TPC
            step = max(min(needed - 3, step - 2), -1)
            qk_at[step] = i

        idle = ps_o.tile([P, W], F32, tag="acc")

        def keep_warm(count):
            for y in range(count):
                nc.tensor.matmul(idle[:], lhsT=zeros[:, 0:P], rhs=zeros[:], start=True, stop=True)

        keep_warm(4)
        transpose_qk(0, 0)
        keep_warm(3)
        copy_qk(0, 0)
        for g in range(NCH):
            regroup_v(0, g)
        for s in range(-2, max(mx_at) + 2):
            odd = s % 2 == 1
            if s in te_at:
                transpose_e(te_at[s])
            if s >= TPC and s % TPC == 0 and has_back(s // TPC - 1):
                transpose_back(s // TPC - 1)
            if s in mx_at:
                e_times_v(mx_at[s])
            if 0 <= s + 2 < NQ:
                near_scores(s + 2)
            if s >= 2 and not odd and has_back((s + TPC) // TPC):
                if s >= TPC:
                    back_scores((s + TPC) // TPC, s % TPC)
                else:
                    back_scores(1, 0)
                    back_scores(1, 2)
            if s in qk_at:
                transpose_qk(*chunks[qk_at[s]])
            if s % TPC == TPC - 1 and has_back((s + 1) // TPC):
                back_max((s + 1) // TPC)
            if 0 <= s + 1 < NQ:
                near_max(s + 1)
            if s > 0 and s - 1 in qk_at:
                copy_qk(*chunks[qk_at[s - 1]])
            if s - 1 in mx_at:
                scale_and_store(mx_at[s - 1])
            if s - 1 in te_at:
                quantise_e(te_at[s - 1])
            if s >= TPC + 1 and s % TPC == 1 and has_back(s // TPC - 1):
                quantise_back(s // TPC - 1)
            if 0 <= s + 1 < NQ:
                bias(s + 1)
            if s % TPC == 1 and 0 < s // TPC < NC:
                invert_row_sums(s - TPC - 1, TPC)
            if s + 1 in mx_at and mx_at[s + 1] >= NQ - TPC:
                invert_row_sums(mx_at[s + 1], size[mx_at[s + 1]])
            if s % TPC == 0 and 0 < s // TPC < NC:
                add_row_sums(s - TPC, TPC)
            if s + 2 in mx_at and mx_at[s + 2] >= NQ - TPC:
                add_row_sums(mx_at[s + 2], size[mx_at[s + 2]])
            if 0 <= s < NQ:
                exponentials(s)
            if s == 0:
                copy_qk(*chunks[1])
            if s in te_at:
                copy_e(te_at[s])
            if s >= TPC and s % TPC == 0 and has_back(s // TPC - 1):
                copy_back(s // TPC - 1)
            if 0 <= s < 2:
                quantise_v(0, 2 * s)
                quantise_v(0, 2 * s + 1)
                if s == 1:
                    move_v(0)
            g = NCH + 1 - s // 3
            if s % 3 == 0 and 0 <= g < NCH:
                regroup_v(1, g)
            g = NCH + 1 - (s - 1) // 3
            if s % 3 == 1 and 0 <= g < NCH:
                quantise_v(1, g)
                if g == 0:
                    move_v(1)
